import numpy as np
import ml_dtypes


def mxq(x, axis, fmt="e4m3"):
    dtype, down = {"e4m3": (ml_dtypes.float8_e4m3fn, 7), "e5m2": (ml_dtypes.float8_e5m2, 14)}[fmt]
    v = np.moveaxis(np.asarray(x, np.float32).astype(ml_dtypes.bfloat16).astype(np.float64), axis, -1)
    blocks = v.reshape(v.shape[:-1] + (-1, 32))
    amax = np.abs(blocks).max(-1, keepdims=True)
    byte = np.maximum(np.where(amax > 0, np.frexp(amax)[1] - 1 + 127, 0) - down, 1)
    scale = np.exp2(byte - 127.0)
    codes = (blocks / scale).astype(np.float32).astype(dtype).astype(np.float64)
    return np.moveaxis((codes * scale).reshape(v.shape), -1, axis)


WIDE = False


def mx_kscale(k):
    if not WIDE:
        return np.ones(k)
    levels = np.array([10, -10, 5, -5, 0])
    if k % 512:
        return np.exp2(np.random.permutation(np.resize(levels, k // 32))).repeat(32)
    a = np.empty((k // 512, 16))
    for p in range(k // 512):
        a[p, :8] = np.random.permutation(np.resize(levels, 8))
        for g in range(8):
            far = levels[np.abs(levels - a[p, g]) >= 10]
            a[p, g + 8] = far[np.random.randint(len(far))]
    return np.exp2(a.ravel()).repeat(32)


BF16 = ml_dtypes.bfloat16


def bf(x):
    return np.asarray(x, np.float32).astype(BF16)


def f64(x):
    return np.asarray(x).astype(np.float64)


N, T, C, D, H, DO = 8, 1024, 1024, 256, 16, 1024
HD = D // H


def head_scores(q, k):
    return np.stack([(q * k[:, :, g:g + 1, :]).sum(-1) for g in range(H)], axis=-1)


def setup_inputs():
    s = mx_kscale(C)
    return {"x": bf(np.random.standard_normal((N, T, C)) * s),
            "w_qk": bf(np.random.standard_normal((C, 2 * D)) / np.sqrt(C) / s[:, None]),
            "b_qk": bf(np.random.standard_normal(2 * D) * 0.3)}


def reference(x, w_qk, b_qk):
    qk = (mxq(f64(x), 2, "e4m3") @ mxq(f64(w_qk), 0, "e4m3")) + f64(b_qk)
    qk = qk.reshape(N, T, 2, H, HD)
    q, k = qk[:, :, 0], qk[:, :, 1]
    s = head_scores(q * HD ** -0.5, k)
    e = np.exp(s - s.max(-1, keepdims=True))
    return e / e.sum(-1, keepdims=True)

@@ -1,0 +1,291 @@
+from contextlib import ExitStack
+
+import concourse.mybir as mybir
+from concourse.masks import make_identity
+
+F32 = mybir.dt.float32
+BF16 = mybir.dt.bfloat16
+U32 = mybir.dt.uint32
+U8 = mybir.dt.uint8
+FP8X4 = mybir.dt.float8_e4m3fn_x4
+ALU = mybir.AluOpType
+ACT = mybir.ActivationFunctionType
+AXIS = mybir.AxisListType
+
+P = 128
+BATCH = 8
+TOKENS = 1024
+K = 1024
+HEADS = 16
+HD = 16
+Q_COLS = HEADS * HD
+QK_COLS = 2 * Q_COLS
+PACK = 4
+PASSES = K // (P * PACK)
+WORD_TILES = K // 2 // P
+TILES = TOKENS // P
+UNITS = BATCH * TILES
+PAIR_BLOCKS = HEADS * HEADS // P
+HEADS_PER_BLOCK = HEADS // PAIR_BLOCKS
+D_ON_GPSIMD = 2
+D_ON_VECTOR = HD - D_ON_GPSIMD
+
+LOAD_AHEAD = 4
+QUANTISE_LAG = 1
+PROJECT_LAG = QUANTISE_LAG + 1
+MULTIPLY_LAG = PROJECT_LAG + 1
+SUM_LAG = MULTIPLY_LAG + 1
+BACK_LAG = SUM_LAG + 1
+SHIFT_LAG = BACK_LAG + 1
+NORMALISE_LAG = SHIFT_LAG + 1
+
+FLOPS = 2 * BATCH * TOKENS * K * QK_COLS + 2 * BATCH * TOKENS * HEADS * HEADS * HD
+
+
+def tile_attention_pa_t_kernel(tc, x, w_qk, b_qk, out):
+    nc = tc.nc
+    with ExitStack() as stack:
+        stack.enter_context(tc.manual_schedule())
+        const = stack.enter_context(tc.tile_pool(name="const", bufs=1))
+        x_pool = stack.enter_context(tc.tile_pool(name="x_pool", bufs=LOAD_AHEAD + 1))
+        work = stack.enter_context(tc.tile_pool(name="work", bufs=2))
+        soft_pool = stack.enter_context(tc.tile_pool(name="soft_pool", bufs=3))
+        gpsimd_pool = stack.enter_context(tc.tile_pool(name="gpsimd_pool", bufs=1))
+        psum_xt = stack.enter_context(tc.psum_pool(name="psum_xt", bufs=2))
+        psum_qk = stack.enter_context(tc.psum_pool(name="psum_qk", bufs=2))
+        psum_sum = stack.enter_context(tc.psum_pool(name="psum_sum", bufs=2))
+        psum_back = stack.enter_context(tc.psum_pool(name="psum_back", bufs=2))
+
+        x_rows_of = {}
+        x_grouped_of = {}
+        x_mx_of = {}
+        qk_sum_of = {}
+        qk_of = {}
+        products_of = {}
+        last_products_of = {}
+        pair_rows_of = {}
+        pair_rows_kept_of = {}
+        score_of = {}
+        top_of = {}
+        shift_of = {}
+        prob_of = {}
+        total_of = {}
+        inverse_of = {}
+
+        def load_x(unit):
+            n, j = divmod(unit, TILES)
+            x_rows = x_pool.tile([P, K], BF16)
+            nc.sync.dma_start(out=x_rows[:], in_=x[n].rearrange("(t j) k -> t j k", j=TILES)[:, j, :])
+            x_rows_of[unit] = x_rows
+
+        load_x(0)
+
+        ident = const.tile([P, P], F32)
+        make_identity(nc, ident[:])
+
+        w_codes = const.tile([P, PASSES, QK_COLS], U32, align_bytes=64)
+        w_scales = const.tile([P, PASSES, QK_COLS], U8, align_bytes=64)
+        for c in range(PASSES):
+            w_rows = const.tile([P, PACK, QK_COLS], BF16, name="w_rows%d" % c)
+            first = c * PACK * P
+            nc.sync.dma_start(
+                out=w_rows[:],
+                in_=w_qk[first : first + PACK * P, :].rearrange("(p v) n -> p v n", v=PACK),
+            )
+            w_grouped = const.tile([P, QK_COLS, PACK], BF16, align_bytes=64, name="w_grouped%d" % c)
+            for half in range(2):
+                cols = slice(half * Q_COLS, (half + 1) * Q_COLS)
+                nc.vector.tensor_copy(
+                    out=w_grouped[:, cols, :].rearrange("p (d h) v -> p d h v", d=HD),
+                    in_=w_rows[:, :, cols].rearrange("p v (h d) -> p d h v", d=HD),
+                )
+            nc.vector.quantize_mx(
+                out=w_codes[:, c, :].bitcast(FP8X4),
+                scales=w_scales[:, c, :],
+                in_=w_grouped[:].rearrange("p n v -> p (n v)"),
+            )
+
+        bias_bf16 = const.tile([P, QK_COLS], BF16)
+        nc.sync.dma_start(out=bias_bf16[:], in_=b_qk.partition_broadcast(P))
+        bias = const.tile([P, QK_COLS], F32)
+        nc.vector.tensor_copy(
+            out=bias[:].rearrange("p (c d h) -> p c d h", c=2, d=HD),
+            in_=bias_bf16[:].rearrange("p (c h d) -> p c d h", c=2, d=HD),
+        )
+
+        for unit in range(1, LOAD_AHEAD):
+            load_x(unit)
+
+        def turn_x(unit):
+            x_words = x_rows_of[unit][:].bitcast(F32)
+            x_turned = psum_xt.tile([P, WORD_TILES, P], F32)
+            for w in range(WORD_TILES):
+                c, u = divmod(w, 2)
+                first = c * 2 * P
+                nc.tensor.transpose(
+                    x_turned[:, w, :], x_words[:, first + u : first + 2 * P : 2], ident[:]
+                )
+            x_grouped = work.tile([P, K], BF16, align_bytes=64)
+            nc.scalar.copy(
+                out=x_grouped[:].bitcast(F32).rearrange("p (c t u) -> p c t u", c=PASSES, u=2),
+                in_=x_turned[:].rearrange("p (c u) t -> p c t u", u=2),
+            )
+            x_grouped_of[unit] = x_grouped
+
+        def quantise_x(unit):
+            x_codes = work.tile([P, PASSES, P], U32, align_bytes=64)
+            x_scales = work.tile([P, PASSES, P], U8, align_bytes=64)
+            nc.vector.quantize_mx(
+                out=x_codes[:].rearrange("p c t -> p (c t)").bitcast(FP8X4),
+                scales=x_scales[:].rearrange("p c t -> p (c t)"),
+                in_=x_grouped_of[unit][:],
+            )
+            x_mx_of[unit] = (x_codes, x_scales)
+
+        def project(unit):
+            x_codes, x_scales = x_mx_of[unit]
+            qk_sum = psum_qk.tile([P, QK_COLS], F32)
+            for c in range(PASSES):
+                nc.tensor.matmul_mx(
+                    out=qk_sum[:],
+                    lhsT=x_codes[:, c, :].bitcast(FP8X4),
+                    lhsT_scale=x_scales[:, c, :],
+                    rhs=w_codes[:, c, :].bitcast(FP8X4),
+                    rhs_scale=w_scales[:, c, :],
+                    start=(c == 0),
+                    stop=(c == PASSES - 1),
+                )
+            qk_sum_of[unit] = qk_sum
+
+        def add_bias(unit):
+            qk = work.tile([P, QK_COLS], F32)
+            nc.vector.tensor_tensor(out=qk[:], in0=qk_sum_of[unit][:], in1=bias[:], op=ALU.add)
+            qk_of[unit] = qk
+
+        def multiply(engine, products, qk, d0, d1):
+            shape = [P, d1 - d0, HEADS, HEADS]
+            engine.tensor_tensor(
+                out=products[:],
+                in0=qk[:, 0:Q_COLS]
+                .rearrange("p (d h) -> p d h", d=HD)[:, d0:d1, :]
+                .unsqueeze(3)
+                .to_broadcast(shape),
+                in1=qk[:, Q_COLS:QK_COLS]
+                .rearrange("p (d g) -> p d g", d=HD)[:, d0:d1, :]
+                .unsqueeze(2)
+                .to_broadcast(shape),
+                op=ALU.mult,
+            )
+
+        def multiply_heads(unit):
+            products = work.tile([P, D_ON_VECTOR, HEADS, HEADS], F32)
+            multiply(nc.vector, products, qk_of[unit], 0, D_ON_VECTOR)
+            products_of[unit] = products
+
+        def multiply_last_d(unit):
+            last_products = gpsimd_pool.tile([P, D_ON_GPSIMD, HEADS, HEADS], F32)
+            multiply(nc.gpsimd, last_products, qk_of[unit], D_ON_VECTOR, HD)
+            last_products_of[unit] = last_products
+
+        def sum_over_d(unit):
+            pair_rows = psum_sum.tile([P, PAIR_BLOCKS, P], F32)
+            for b in range(PAIR_BLOCKS):
+                h0 = b * HEADS_PER_BLOCK
+                for d in range(HD):
+                    if d < D_ON_VECTOR:
+                        of_d = products_of[unit][:, d, :, :]
+                    else:
+                        of_d = last_products_of[unit][:, d - D_ON_VECTOR, :, :]
+                    nc.tensor.matmul(
+                        out=pair_rows[:, b, :],
+                        lhsT=of_d[:, h0 : h0 + HEADS_PER_BLOCK, :].rearrange("p h g -> p (h g)"),
+                        rhs=ident[:],
+                        is_transpose=True,
+                        start=(d == 0),
+                        stop=(d == HD - 1),
+                    )
+            pair_rows_of[unit] = pair_rows
+
+        def keep_pair_rows(unit):
+            pair_rows_kept = work.tile([P, PAIR_BLOCKS, P], F32)
+            nc.scalar.copy(out=pair_rows_kept[:], in_=pair_rows_of[unit][:])
+            pair_rows_kept_of[unit] = pair_rows_kept
+
+        def turn_back(unit):
+            score = psum_back.tile([P, HEADS, HEADS], F32)
+            for b in range(PAIR_BLOCKS):
+                h0 = b * HEADS_PER_BLOCK
+                nc.tensor.transpose(
+                    score[:, h0 : h0 + HEADS_PER_BLOCK, :].rearrange("p h g -> p (h g)"),
+                    pair_rows_kept_of[unit][:, b, :],
+                    ident[:],
+                )
+            score_of[unit] = score
+
+        def find_top(unit):
+            top = soft_pool.tile([P, HEADS], F32)
+            nc.vector.tensor_reduce(out=top[:], in_=score_of[unit][:], axis=AXIS.X, op=ALU.max)
+            top_of[unit] = top
+
+        def negate_top(unit):
+            shift = soft_pool.tile([P, HEADS], F32)
+            nc.vector.tensor_scalar(
+                out=shift[:], in0=top_of[unit][:], scalar1=-(HD**-0.5), scalar2=None, op0=ALU.mult
+            )
+            shift_of[unit] = shift
+
+        def exponential(unit):
+            prob = soft_pool.tile([P, HEADS, HEADS], F32)
+            total = soft_pool.tile([P, HEADS], F32)
+            for h in range(HEADS):
+                nc.scalar.activation(
+                    out=prob[:, h, :],
+                    in_=score_of[unit][:, h, :],
+                    func=ACT.Exp,
+                    bias=shift_of[unit][:, h : h + 1],
+                    scale=HD**-0.5,
+                    accum_out=total[:, h : h + 1],
+                )
+            prob_of[unit] = prob
+            total_of[unit] = total
+
+        def invert(unit):
+            inverse = soft_pool.tile([P, HEADS], F32)
+            nc.vector.reciprocal(out=inverse[:], in_=total_of[unit][:])
+            inverse_of[unit] = inverse
+
+        def scale_and_store(unit):
+            n, j = divmod(unit, TILES)
+            prob = prob_of[unit]
+            for h in range(HEADS):
+                nc.scalar.activation(
+                    out=prob[:, h, :],
+                    in_=prob[:, h, :],
+                    func=ACT.Copy,
+                    scale=inverse_of[unit][:, h : h + 1],
+                )
+            nc.sync.dma_start(
+                out=out[n].rearrange("(t j) h g -> t j (h g)", j=TILES)[:, j, :],
+                in_=prob[:].rearrange("p h g -> p (h g)"),
+            )
+
+        def run(stage, unit):
+            if 0 <= unit < UNITS:
+                stage(unit)
+
+        for step in range(UNITS + NORMALISE_LAG):
+            run(load_x, step + LOAD_AHEAD)
+            run(multiply_last_d, step - SUM_LAG)
+            run(keep_pair_rows, step - BACK_LAG)
+            run(project, step - PROJECT_LAG)
+            run(find_top, step - SHIFT_LAG)
+            run(add_bias, step - MULTIPLY_LAG)
+            run(negate_top, step - SHIFT_LAG)
+            run(exponential, step - SHIFT_LAG)
+            run(invert, step - NORMALISE_LAG)
+            run(quantise_x, step - QUANTISE_LAG)
+            run(multiply_heads, step - MULTIPLY_LAG)
+            run(turn_x, step)
+            run(scale_and_store, step - NORMALISE_LAG)
+            run(sum_over_d, step - SUM_LAG)
+            run(turn_back, step - BACK_LAG)

@@ -27,8 +27,9 @@ TILES = TOKENS // P
 UNITS = BATCH * TILES
 PAIR_BLOCKS = HEADS * HEADS // P
 HEADS_PER_BLOCK = HEADS // PAIR_BLOCKS
-D_ON_GPSIMD = 2
+D_ON_GPSIMD = 5
 D_ON_VECTOR = HD - D_ON_GPSIMD
+Q_BLOCKS = Q_COLS // P
 
 LOAD_AHEAD = 4
 QUANTISE_LAG = 1
@@ -50,24 +51,28 @@ def tile_attention_pa_t_kernel(tc, x, w_qk, b_qk, out):
         x_pool = stack.enter_context(tc.tile_pool(name="x_pool", bufs=LOAD_AHEAD + 1))
         work = stack.enter_context(tc.tile_pool(name="work", bufs=2))
         soft_pool = stack.enter_context(tc.tile_pool(name="soft_pool", bufs=3))
-        gpsimd_pool = stack.enter_context(tc.tile_pool(name="gpsimd_pool", bufs=1))
-        psum_xt = stack.enter_context(tc.psum_pool(name="psum_xt", bufs=2))
-        psum_qk = stack.enter_context(tc.psum_pool(name="psum_qk", bufs=2))
+        psum_xt = stack.enter_context(tc.psum_pool(name="psum_xt", bufs=1))
+        psum_q_rows = stack.enter_context(tc.psum_pool(name="psum_q_rows", bufs=1))
+        psum_k = stack.enter_context(tc.psum_pool(name="psum_k", bufs=1))
+        psum_q = stack.enter_context(tc.psum_pool(name="psum_q", bufs=2))
         psum_sum = stack.enter_context(tc.psum_pool(name="psum_sum", bufs=2))
-        psum_back = stack.enter_context(tc.psum_pool(name="psum_back", bufs=2))
+        psum_back = stack.enter_context(tc.psum_pool(name="psum_back", bufs=1))
 
         x_rows_of = {}
         x_grouped_of = {}
         x_mx_of = {}
-        qk_sum_of = {}
-        qk_of = {}
+        q_rows_sum_of = {}
+        q_rows_of = {}
+        q_of = {}
+        q_kept_of = {}
+        k_sum_of = {}
+        k_of = {}
         products_of = {}
         last_products_of = {}
         pair_rows_of = {}
         pair_rows_kept_of = {}
         score_of = {}
-        top_of = {}
-        shift_of = {}
+        low_of = {}
         prob_of = {}
         total_of = {}
         inverse_of = {}
@@ -113,6 +118,14 @@ def tile_attention_pa_t_kernel(tc, x, w_qk, b_qk, out):
             in_=bias_bf16[:].rearrange("p (c h d) -> p c d h", c=2, d=HD),
         )
 
+        bias_rows = psum_q.tile([P, Q_BLOCKS, P], F32, name="q")
+        q_bias = const.tile([P, Q_BLOCKS], F32)
+        for b in range(Q_BLOCKS):
+            nc.tensor.transpose(bias_rows[:, b, :], bias[:, b * P : (b + 1) * P], ident[:])
+        nc.scalar.activation(
+            out=q_bias[:], in_=bias_rows[:, :, 0], func=ACT.Copy, scale=-(HD**-0.5)
+        )
+
         for unit in range(1, LOAD_AHEAD):
             load_x(unit)
 
@@ -144,47 +157,81 @@ def tile_attention_pa_t_kernel(tc, x, w_qk, b_qk, out):
 
         def project(unit):
             x_codes, x_scales = x_mx_of[unit]
-            qk_sum = psum_qk.tile([P, QK_COLS], F32)
+            q_rows_sum = psum_q_rows.tile([P, Q_BLOCKS, P], F32)
+            for b in range(Q_BLOCKS):
+                for c in range(PASSES):
+                    nc.tensor.matmul_mx(
+                        out=q_rows_sum[:, b, :],
+                        lhsT=w_codes[:, c, b * P : (b + 1) * P].bitcast(FP8X4),
+                        lhsT_scale=w_scales[:, c, b * P : (b + 1) * P],
+                        rhs=x_codes[:, c, :].bitcast(FP8X4),
+                        rhs_scale=x_scales[:, c, :],
+                        start=(c == 0),
+                        stop=(c == PASSES - 1),
+                    )
+            q_rows_sum_of[unit] = q_rows_sum
+            k_sum = psum_k.tile([P, Q_COLS], F32)
             for c in range(PASSES):
                 nc.tensor.matmul_mx(
-                    out=qk_sum[:],
+                    out=k_sum[:],
                     lhsT=x_codes[:, c, :].bitcast(FP8X4),
                     lhsT_scale=x_scales[:, c, :],
-                    rhs=w_codes[:, c, :].bitcast(FP8X4),
-                    rhs_scale=w_scales[:, c, :],
+                    rhs=w_codes[:, c, Q_COLS:QK_COLS].bitcast(FP8X4),
+                    rhs_scale=w_scales[:, c, Q_COLS:QK_COLS],
                     start=(c == 0),
                     stop=(c == PASSES - 1),
                 )
-            qk_sum_of[unit] = qk_sum
+            k_sum_of[unit] = k_sum
 
-        def add_bias(unit):
-            qk = work.tile([P, QK_COLS], F32)
-            nc.vector.tensor_tensor(out=qk[:], in0=qk_sum_of[unit][:], in1=bias[:], op=ALU.add)
-            qk_of[unit] = qk
+        def add_q_bias(unit):
+            q_rows = work.tile([P, Q_BLOCKS, P], F32)
+            for b in range(Q_BLOCKS):
+                nc.scalar.activation(
+                    out=q_rows[:, b, :],
+                    in_=q_rows_sum_of[unit][:, b, :],
+                    func=ACT.Identity,
+                    bias=q_bias[:, b : b + 1],
+                    scale=-(HD**-0.5),
+                )
+            q_rows_of[unit] = q_rows
 
-        def multiply(engine, products, qk, d0, d1):
-            shape = [P, d1 - d0, HEADS, HEADS]
+        def turn_q(unit):
+            q = psum_q.tile([P, Q_COLS], F32)
+            for b in range(Q_BLOCKS):
+                nc.tensor.transpose(q[:, b * P : (b + 1) * P], q_rows_of[unit][:, b, :], ident[:])
+            q_of[unit] = q
+
+        def keep_last_q(unit):
+            q_kept = work.tile([P, D_ON_GPSIMD * HEADS], F32)
+            nc.scalar.copy(out=q_kept[:], in_=q_of[unit][:, D_ON_VECTOR * HEADS :])
+            q_kept_of[unit] = q_kept
+
+        def add_k_bias(unit):
+            k = work.tile([P, Q_COLS], F32)
+            nc.vector.tensor_tensor(
+                out=k[:], in0=k_sum_of[unit][:], in1=bias[:, Q_COLS:QK_COLS], op=ALU.add
+            )
+            k_of[unit] = k
+
+        def multiply(engine, products, q, k, count):
+            shape = [P, count, HEADS, HEADS]
             engine.tensor_tensor(
                 out=products[:],
-                in0=qk[:, 0:Q_COLS]
-                .rearrange("p (d h) -> p d h", d=HD)[:, d0:d1, :]
-                .unsqueeze(3)
-                .to_broadcast(shape),
-                in1=qk[:, Q_COLS:QK_COLS]
-                .rearrange("p (d g) -> p d g", d=HD)[:, d0:d1, :]
-                .unsqueeze(2)
-                .to_broadcast(shape),
+                in0=q.rearrange("p (d h) -> p d h", d=count).unsqueeze(3).to_broadcast(shape),
+                in1=k.rearrange("p (d g) -> p d g", d=count).unsqueeze(2).to_broadcast(shape),
                 op=ALU.mult,
             )
 
         def multiply_heads(unit):
             products = work.tile([P, D_ON_VECTOR, HEADS, HEADS], F32)
-            multiply(nc.vector, products, qk_of[unit], 0, D_ON_VECTOR)
+            cols = slice(0, D_ON_VECTOR * HEADS)
+            multiply(nc.vector, products, q_of[unit][:, cols], k_of[unit][:, cols], D_ON_VECTOR)
             products_of[unit] = products
 
         def multiply_last_d(unit):
-            last_products = gpsimd_pool.tile([P, D_ON_GPSIMD, HEADS, HEADS], F32)
-            multiply(nc.gpsimd, last_products, qk_of[unit], D_ON_VECTOR, HD)
+            last_products = work.tile([P, D_ON_GPSIMD, HEADS, HEADS], F32)
+            cols = slice(D_ON_VECTOR * HEADS, Q_COLS)
+            multiply(nc.gpsimd, last_products, q_kept_of[unit][:], k_of[unit][:, cols], D_ON_GPSIMD)
             last_products_of[unit] = last_products
 
         def sum_over_d(unit):
@@ -222,17 +269,10 @@ def tile_attention_pa_t_kernel(tc, x, w_qk, b_qk, out):
                 )
             score_of[unit] = score
 
-        def find_top(unit):
-            top = soft_pool.tile([P, HEADS], F32)
-            nc.vector.tensor_reduce(out=top[:], in_=score_of[unit][:], axis=AXIS.X, op=ALU.max)
-            top_of[unit] = top
-
-        def negate_top(unit):
-            shift = soft_pool.tile([P, HEADS], F32)
-            nc.vector.tensor_scalar(
-                out=shift[:], in0=top_of[unit][:], scalar1=-(HD**-0.5), scalar2=None, op0=ALU.mult
-            )
-            shift_of[unit] = shift
+        def find_low(unit):
+            low = soft_pool.tile([P, HEADS], F32)
+            nc.vector.tensor_reduce(out=low[:], in_=score_of[unit][:], axis=AXIS.X, op=ALU.min)
+            low_of[unit] = low
 
         def exponential(unit):
             prob = soft_pool.tile([P, HEADS, HEADS], F32)
@@ -242,8 +282,8 @@ def tile_attention_pa_t_kernel(tc, x, w_qk, b_qk, out):
                     out=prob[:, h, :],
                     in_=score_of[unit][:, h, :],
                     func=ACT.Exp,
-                    bias=shift_of[unit][:, h : h + 1],
-                    scale=HD**-0.5,
+                    bias=low_of[unit][:, h : h + 1],
+                    scale=-1.0,
                     accum_out=total[:, h : h + 1],
                 )
             prob_of[unit] = prob
@@ -275,16 +315,18 @@ def tile_attention_pa_t_kernel(tc, x, w_qk, b_qk, out):
 
         for step in range(UNITS + NORMALISE_LAG):
             run(load_x, step + LOAD_AHEAD)
-            run(multiply_last_d, step - SUM_LAG)
+            run(turn_q, step - MULTIPLY_LAG)
             run(keep_pair_rows, step - BACK_LAG)
-            run(project, step - PROJECT_LAG)
-            run(find_top, step - SHIFT_LAG)
-            run(add_bias, step - MULTIPLY_LAG)
-            run(negate_top, step - SHIFT_LAG)
-            run(exponential, step - SHIFT_LAG)
+            run(keep_last_q, step - MULTIPLY_LAG)
             run(invert, step - NORMALISE_LAG)
             run(quantise_x, step - QUANTISE_LAG)
+            run(add_k_bias, step - MULTIPLY_LAG)
+            run(multiply_last_d, step - MULTIPLY_LAG)
+            run(find_low, step - SHIFT_LAG)
             run(multiply_heads, step - MULTIPLY_LAG)
+            run(project, step - PROJECT_LAG)
+            run(add_q_bias, step - PROJECT_LAG)
+            run(exponential, step - SHIFT_LAG)
             run(turn_x, step)
             run(scale_and_store, step - NORMALISE_LAG)
             run(sum_over_d, step - SUM_LAG)

@@ -27,7 +27,7 @@ TILES = TOKENS // P
 UNITS = BATCH * TILES
 PAIR_BLOCKS = HEADS * HEADS // P
 HEADS_PER_BLOCK = HEADS // PAIR_BLOCKS
-D_ON_GPSIMD = 5
+D_ON_GPSIMD = 6
 D_ON_VECTOR = HD - D_ON_GPSIMD
 Q_BLOCKS = Q_COLS // P
 
@@ -90,6 +90,7 @@ def tile_attention_pa_t_kernel(tc, x, w_qk, b_qk, out):
 
         w_codes = const.tile([P, PASSES, QK_COLS], U32, align_bytes=64)
         w_scales = const.tile([P, PASSES, QK_COLS], U8, align_bytes=64)
+        w_rows_of = {}
         for c in range(PASSES):
             w_rows = const.tile([P, PACK, QK_COLS], BF16, name="w_rows%d" % c)
             first = c * PACK * P
@@ -97,37 +98,37 @@ def tile_attention_pa_t_kernel(tc, x, w_qk, b_qk, out):
                 out=w_rows[:],
                 in_=w_qk[first : first + PACK * P, :].rearrange("(p v) n -> p v n", v=PACK),
             )
-            w_grouped = const.tile([P, QK_COLS, PACK], BF16, align_bytes=64, name="w_grouped%d" % c)
-            for half in range(2):
-                cols = slice(half * Q_COLS, (half + 1) * Q_COLS)
-                nc.vector.tensor_copy(
-                    out=w_grouped[:, cols, :].rearrange("p (d h) v -> p d h v", d=HD),
-                    in_=w_rows[:, :, cols].rearrange("p v (h d) -> p d h v", d=HD),
-                )
-            nc.vector.quantize_mx(
-                out=w_codes[:, c, :].bitcast(FP8X4),
-                scales=w_scales[:, c, :],
-                in_=w_grouped[:].rearrange("p n v -> p (n v)"),
-            )
-
+            w_rows_of[c] = w_rows
         bias_bf16 = const.tile([P, QK_COLS], BF16)
         nc.sync.dma_start(out=bias_bf16[:], in_=b_qk.partition_broadcast(P))
         bias = const.tile([P, QK_COLS], F32)
-        nc.vector.tensor_copy(
-            out=bias[:].rearrange("p (c d h) -> p c d h", c=2, d=HD),
-            in_=bias_bf16[:].rearrange("p (c h d) -> p c d h", c=2, d=HD),
-        )
-
-        bias_rows = psum_q.tile([P, Q_BLOCKS, P], F32, name="q")
         q_bias = const.tile([P, Q_BLOCKS], F32)
-        for b in range(Q_BLOCKS):
-            nc.tensor.transpose(bias_rows[:, b, :], bias[:, b * P : (b + 1) * P], ident[:])
-        nc.scalar.activation(
-            out=q_bias[:], in_=bias_rows[:, :, 0], func=ACT.Copy, scale=-(HD**-0.5)
-        )
 
         for unit in range(1, LOAD_AHEAD):
             load_x(unit)
+
+        def prepare_weights():
+            for c in range(PASSES):
+                w_grouped = const.tile(
+                    [P, QK_COLS, PACK], BF16, align_bytes=64, name="w_grouped%d" % c
+                )
+                for half in range(2):
+                    cols = slice(half * Q_COLS, (half + 1) * Q_COLS)
+                    on_scalar = c == PASSES - 1 and half == 1
+                    copy = nc.scalar.copy if on_scalar else nc.vector.tensor_copy
+                    copy(
+                        out=w_grouped[:, cols, :].rearrange("p (d h) v -> p d h v", d=HD),
+                        in_=w_rows_of[c][:, :, cols].rearrange("p v (h d) -> p d h v", d=HD),
+                    )
+                nc.vector.quantize_mx(
+                    out=w_codes[:, c, :].bitcast(FP8X4),
+                    scales=w_scales[:, c, :],
+                    in_=w_grouped[:].rearrange("p n v -> p (n v)"),
+                )
+            nc.scalar.copy(
+                out=bias[:].rearrange("p (c d h) -> p c d h", c=2, d=HD),
+                in_=bias_bf16[:].rearrange("p (c h d) -> p c d h", c=2, d=HD),
+            )
 
         def turn_x(unit):
             x_words = x_rows_of[unit][:].bitcast(F32)
@@ -182,6 +183,14 @@ def tile_attention_pa_t_kernel(tc, x, w_qk, b_qk, out):
                     stop=(c == PASSES - 1),
                 )
             k_sum_of[unit] = k_sum
+
+        def make_q_bias():
+            bias_rows = psum_q.tile([P, Q_BLOCKS, P], F32, name="q")
+            for b in range(Q_BLOCKS):
+                nc.tensor.transpose(bias_rows[:, b, :], bias[:, b * P : (b + 1) * P], ident[:])
+            nc.scalar.activation(
+                out=q_bias[:], in_=bias_rows[:, :, 0], func=ACT.Copy, scale=-(HD**-0.5)
+            )
 
         def add_q_bias(unit):
             q_rows = work.tile([P, Q_BLOCKS, P], F32)
@@ -325,9 +334,13 @@ def tile_attention_pa_t_kernel(tc, x, w_qk, b_qk, out):
             run(find_low, step - SHIFT_LAG)
             run(multiply_heads, step - MULTIPLY_LAG)
             run(project, step - PROJECT_LAG)
+            if step == PROJECT_LAG:
+                make_q_bias()
             run(add_q_bias, step - PROJECT_LAG)
             run(exponential, step - SHIFT_LAG)
             run(turn_x, step)
+            if step == 0:
+                prepare_weights()
             run(scale_and_store, step - NORMALISE_LAG)
             run(sum_over_d, step - SUM_LAG)
             run(turn_back, step - BACK_LAG)

@@ -31,8 +31,10 @@ D_ON_GPSIMD = 6
 D_ON_VECTOR = HD - D_ON_GPSIMD
 Q_BLOCKS = Q_COLS // P
 
+PAIR = 2
+
 LOAD_AHEAD = 4
-QUANTISE_LAG = 1
+QUANTISE_LAG = PAIR
 PROJECT_LAG = QUANTISE_LAG + 1
 MULTIPLY_LAG = PROJECT_LAG + 1
 SUM_LAG = MULTIPLY_LAG + 1
@@ -139,26 +141,29 @@ def tile_attention_pa_t_kernel(tc, x, w_qk, b_qk, out):
                 nc.tensor.transpose(
                     x_turned[:, w, :], x_words[:, first + u : first + 2 * P : 2], ident[:]
                 )
-            x_grouped = work.tile([P, K], BF16, align_bytes=64)
+            if unit % PAIR == 0:
+                x_grouped = work.tile([P, PASSES, PAIR, P * PACK], BF16, align_bytes=64)
+                x_grouped_of[unit // PAIR] = x_grouped
             nc.scalar.copy(
-                out=x_grouped[:].bitcast(F32).rearrange("p (c t u) -> p c t u", c=PASSES, u=2),
+                out=x_grouped_of[unit // PAIR][:, :, unit % PAIR, :]
+                .bitcast(F32)
+                .rearrange("p c (t u) -> p c t u", u=2),
                 in_=x_turned[:].rearrange("p (c u) t -> p c t u", u=2),
             )
-            x_grouped_of[unit] = x_grouped
 
-        def quantise_x(unit):
-            x_codes = work.tile([P, PASSES, P], U32, align_bytes=64)
-            x_scales = work.tile([P, PASSES, P], U8, align_bytes=64)
+        def quantise_x(pair):
+            x_codes = work.tile([P, PASSES, PAIR * P], U32, align_bytes=64)
+            x_scales = work.tile([P, PASSES, PAIR * P], U8, align_bytes=64)
             nc.vector.quantize_mx(
                 out=x_codes[:].rearrange("p c t -> p (c t)").bitcast(FP8X4),
                 scales=x_scales[:].rearrange("p c t -> p (c t)"),
-                in_=x_grouped_of[unit][:],
+                in_=x_grouped_of[pair][:].rearrange("p c j w -> p (c j w)"),
             )
-            x_mx_of[unit] = (x_codes, x_scales)
+            x_mx_of[pair] = (x_codes, x_scales)
 
-        def project(unit):
-            x_codes, x_scales = x_mx_of[unit]
-            q_rows_sum = psum_q_rows.tile([P, Q_BLOCKS, P], F32)
+        def project(pair):
+            x_codes, x_scales = x_mx_of[pair]
+            q_rows_sum = psum_q_rows.tile([P, Q_BLOCKS, PAIR * P], F32)
             for b in range(Q_BLOCKS):
                 for c in range(PASSES):
                     nc.tensor.matmul_mx(
@@ -170,19 +175,20 @@ def tile_attention_pa_t_kernel(tc, x, w_qk, b_qk, out):
                         start=(c == 0),
                         stop=(c == PASSES - 1),
                     )
-            q_rows_sum_of[unit] = q_rows_sum
-            k_sum = psum_k.tile([P, Q_COLS], F32)
-            for c in range(PASSES):
-                nc.tensor.matmul_mx(
-                    out=k_sum[:],
-                    lhsT=x_codes[:, c, :].bitcast(FP8X4),
-                    lhsT_scale=x_scales[:, c, :],
-                    rhs=w_codes[:, c, Q_COLS:QK_COLS].bitcast(FP8X4),
-                    rhs_scale=w_scales[:, c, Q_COLS:QK_COLS],
-                    start=(c == 0),
-                    stop=(c == PASSES - 1),
-                )
-            k_sum_of[unit] = k_sum
+            q_rows_sum_of[pair] = q_rows_sum
+            k_sum = psum_k.tile([P, PAIR, Q_COLS], F32)
+            for j in range(PAIR):
+                for c in range(PASSES):
+                    nc.tensor.matmul_mx(
+                        out=k_sum[:, j, :],
+                        lhsT=x_codes[:, c, j * P : (j + 1) * P].bitcast(FP8X4),
+                        lhsT_scale=x_scales[:, c, j * P : (j + 1) * P],
+                        rhs=w_codes[:, c, Q_COLS:QK_COLS].bitcast(FP8X4),
+                        rhs_scale=w_scales[:, c, Q_COLS:QK_COLS],
+                        start=(c == 0),
+                        stop=(c == PASSES - 1),
+                    )
+            k_sum_of[pair] = k_sum
 
         def make_q_bias():
             bias_rows = psum_q.tile([P, Q_BLOCKS, P], F32, name="q")
@@ -192,22 +198,25 @@ def tile_attention_pa_t_kernel(tc, x, w_qk, b_qk, out):
                 out=q_bias[:], in_=bias_rows[:, :, 0], func=ACT.Copy, scale=-(HD**-0.5)
             )
 
-        def add_q_bias(unit):
-            q_rows = work.tile([P, Q_BLOCKS, P], F32)
+        def add_q_bias(pair):
+            q_rows = work.tile([P, Q_BLOCKS, PAIR * P], F32)
             for b in range(Q_BLOCKS):
                 nc.scalar.activation(
                     out=q_rows[:, b, :],
-                    in_=q_rows_sum_of[unit][:, b, :],
+                    in_=q_rows_sum_of[pair][:, b, :],
                     func=ACT.Identity,
                     bias=q_bias[:, b : b + 1],
                     scale=-(HD**-0.5),
                 )
-            q_rows_of[unit] = q_rows
+            q_rows_of[pair] = q_rows
 
         def turn_q(unit):
             q = psum_q.tile([P, Q_COLS], F32)
+            tokens = slice(unit % PAIR * P, (unit % PAIR + 1) * P)
             for b in range(Q_BLOCKS):
-                nc.tensor.transpose(q[:, b * P : (b + 1) * P], q_rows_of[unit][:, b, :], ident[:])
+                nc.tensor.transpose(
+                    q[:, b * P : (b + 1) * P], q_rows_of[unit // PAIR][:, b, tokens], ident[:]
+                )
             q_of[unit] = q
 
         def keep_last_q(unit):
@@ -215,12 +224,15 @@ def tile_attention_pa_t_kernel(tc, x, w_qk, b_qk, out):
             nc.scalar.copy(out=q_kept[:], in_=q_of[unit][:, D_ON_VECTOR * HEADS :])
             q_kept_of[unit] = q_kept
 
-        def add_k_bias(unit):
-            k = work.tile([P, Q_COLS], F32)
+        def add_k_bias(pair):
+            k = work.tile([P, PAIR, Q_COLS], F32)
             nc.vector.tensor_tensor(
-                out=k[:], in0=k_sum_of[unit][:], in1=bias[:, Q_COLS:QK_COLS], op=ALU.add
+                out=k[:],
+                in0=k_sum_of[pair][:],
+                in1=bias[:, Q_COLS:QK_COLS].unsqueeze(1).to_broadcast([P, PAIR, Q_COLS]),
+                op=ALU.add,
             )
-            k_of[unit] = k
+            k_of[pair] = k
 
         def multiply(engine, products, q, k, count):
             shape = [P, count, HEADS, HEADS]
@@ -234,13 +246,15 @@ def tile_attention_pa_t_kernel(tc, x, w_qk, b_qk, out):
         def multiply_heads(unit):
             products = work.tile([P, D_ON_VECTOR, HEADS, HEADS], F32)
             cols = slice(0, D_ON_VECTOR * HEADS)
-            multiply(nc.vector, products, q_of[unit][:, cols], k_of[unit][:, cols], D_ON_VECTOR)
+            k = k_of[unit // PAIR][:, unit % PAIR, cols]
+            multiply(nc.vector, products, q_of[unit][:, cols], k, D_ON_VECTOR)
             products_of[unit] = products
 
         def multiply_last_d(unit):
             last_products = work.tile([P, D_ON_GPSIMD, HEADS, HEADS], F32)
             cols = slice(D_ON_VECTOR * HEADS, Q_COLS)
-            multiply(nc.gpsimd, last_products, q_kept_of[unit][:], k_of[unit][:, cols], D_ON_GPSIMD)
+            k = k_of[unit // PAIR][:, unit % PAIR, cols]
+            multiply(nc.gpsimd, last_products, q_kept_of[unit][:], k, D_ON_GPSIMD)
             last_products_of[unit] = last_products
 
         def sum_over_d(unit):
@@ -322,21 +336,25 @@ def tile_attention_pa_t_kernel(tc, x, w_qk, b_qk, out):
             if 0 <= unit < UNITS:
                 stage(unit)
 
+        def run_pair(stage, unit):
+            if 0 <= unit < UNITS and unit % PAIR == 0:
+                stage(unit // PAIR)
+
         for step in range(UNITS + NORMALISE_LAG):
             run(load_x, step + LOAD_AHEAD)
             run(turn_q, step - MULTIPLY_LAG)
             run(keep_pair_rows, step - BACK_LAG)
             run(keep_last_q, step - MULTIPLY_LAG)
             run(invert, step - NORMALISE_LAG)
-            run(quantise_x, step - QUANTISE_LAG)
-            run(add_k_bias, step - MULTIPLY_LAG)
+            run_pair(add_k_bias, step - MULTIPLY_LAG)
+            run_pair(quantise_x, step - QUANTISE_LAG)
             run(multiply_last_d, step - MULTIPLY_LAG)
             run(find_low, step - SHIFT_LAG)
             run(multiply_heads, step - MULTIPLY_LAG)
-            run(project, step - PROJECT_LAG)
+            run_pair(project, step - PROJECT_LAG)
             if step == PROJECT_LAG:
                 make_q_bias()
-            run(add_q_bias, step - PROJECT_LAG)
+            run_pair(add_q_bias, step - PROJECT_LAG)
             run(exponential, step - SHIFT_LAG)
             run(turn_x, step)
             if step == 0:

@@ -27,7 +27,7 @@ TILES = TOKENS // P
 UNITS = BATCH * TILES
 PAIR_BLOCKS = HEADS * HEADS // P
 HEADS_PER_BLOCK = HEADS // PAIR_BLOCKS
-D_ON_GPSIMD = 6
+D_ON_GPSIMD = 5
 D_ON_VECTOR = HD - D_ON_GPSIMD
 Q_BLOCKS = Q_COLS // P
 

@@ -34,6 +34,7 @@ Q_BLOCKS = Q_COLS // P
 PAIR = 2
 
 LOAD_AHEAD = 4
+SORT_AHEAD = 1
 QUANTISE_LAG = PAIR
 PROJECT_LAG = QUANTISE_LAG + 1
 MULTIPLY_LAG = PROJECT_LAG + 1
@@ -61,6 +62,7 @@ def tile_attention_pa_t_kernel(tc, x, w_qk, b_qk, out):
         psum_back = stack.enter_context(tc.psum_pool(name="psum_back", bufs=1))
 
         x_rows_of = {}
+        x_sorted_of = {}
         x_grouped_of = {}
         x_mx_of = {}
         q_rows_sum_of = {}
@@ -132,15 +134,19 @@ def tile_attention_pa_t_kernel(tc, x, w_qk, b_qk, out):
                 in_=bias_bf16[:].rearrange("p (c h d) -> p c d h", c=2, d=HD),
             )
 
+        def sort_x(unit):
+            x_sorted = work.tile([P, PASSES, 2, P], F32)
+            nc.scalar.copy(
+                out=x_sorted[:],
+                in_=x_rows_of[unit][:].bitcast(F32).rearrange("t (c p u) -> t c u p", c=PASSES, u=2),
+            )
+            x_sorted_of[unit] = x_sorted
+
         def turn_x(unit):
-            x_words = x_rows_of[unit][:].bitcast(F32)
             x_turned = psum_xt.tile([P, WORD_TILES, P], F32)
             for w in range(WORD_TILES):
                 c, u = divmod(w, 2)
-                first = c * 2 * P
-                nc.tensor.transpose(
-                    x_turned[:, w, :], x_words[:, first + u : first + 2 * P : 2], ident[:]
-                )
+                nc.tensor.transpose(x_turned[:, w, :], x_sorted_of[unit][:, c, u, :], ident[:])
             if unit % PAIR == 0:
                 x_grouped = work.tile([P, PASSES, PAIR, P * PACK], BF16, align_bytes=64)
                 x_grouped_of[unit // PAIR] = x_grouped
@@ -340,6 +346,7 @@ def tile_attention_pa_t_kernel(tc, x, w_qk, b_qk, out):
             if 0 <= unit < UNITS and unit % PAIR == 0:
                 stage(unit // PAIR)
 
+        sort_x(0)
         for step in range(UNITS + NORMALISE_LAG):
             run(load_x, step + LOAD_AHEAD)
             run(turn_q, step - MULTIPLY_LAG)
@@ -359,6 +366,7 @@ def tile_attention_pa_t_kernel(tc, x, w_qk, b_qk, out):
             run(turn_x, step)
             if step == 0:
                 prepare_weights()
+            run(sort_x, step + SORT_AHEAD)
             run(scale_and_store, step - NORMALISE_LAG)
             run(sum_over_d, step - SUM_LAG)
             run(turn_back, step - BACK_LAG)

@@ -58,7 +58,7 @@ def tile_attention_pa_t_kernel(tc, x, w_qk, b_qk, out):
         psum_q_rows = stack.enter_context(tc.psum_pool(name="psum_q_rows", bufs=1))
         psum_k = stack.enter_context(tc.psum_pool(name="psum_k", bufs=1))
         psum_q = stack.enter_context(tc.psum_pool(name="psum_q", bufs=2))
-        psum_sum = stack.enter_context(tc.psum_pool(name="psum_sum", bufs=2))
+        psum_sum = stack.enter_context(tc.psum_pool(name="psum_sum", bufs=1))
         psum_back = stack.enter_context(tc.psum_pool(name="psum_back", bufs=1))
 
         x_rows_of = {}
@@ -264,16 +264,18 @@ def tile_attention_pa_t_kernel(tc, x, w_qk, b_qk, out):
             last_products_of[unit] = last_products
 
         def sum_over_d(unit):
-            pair_rows = psum_sum.tile([P, PAIR_BLOCKS, P], F32)
-            for b in range(PAIR_BLOCKS):
-                h0 = b * HEADS_PER_BLOCK
-                for d in range(HD):
-                    if d < D_ON_VECTOR:
-                        of_d = products_of[unit][:, d, :, :]
-                    else:
-                        of_d = last_products_of[unit][:, d - D_ON_VECTOR, :, :]
+            pair_rows = [
+                psum_sum.tile([P, P], F32, name="pair_rows%d" % b) for b in range(PAIR_BLOCKS)
+            ]
+            for d in range(HD):
+                if d < D_ON_VECTOR:
+                    of_d = products_of[unit][:, d, :, :]
+                else:
+                    of_d = last_products_of[unit][:, d - D_ON_VECTOR, :, :]
+                for b in range(PAIR_BLOCKS):
+                    h0 = b * HEADS_PER_BLOCK
                     nc.tensor.matmul(
-                        out=pair_rows[:, b, :],
+                        out=pair_rows[b][:],
                         lhsT=of_d[:, h0 : h0 + HEADS_PER_BLOCK, :].rearrange("p h g -> p (h g)"),
                         rhs=ident[:],
                         is_transpose=True,
@@ -284,7 +286,8 @@ def tile_attention_pa_t_kernel(tc, x, w_qk, b_qk, out):
 
         def keep_pair_rows(unit):
             pair_rows_kept = work.tile([P, PAIR_BLOCKS, P], F32)
-            nc.scalar.copy(out=pair_rows_kept[:], in_=pair_rows_of[unit][:])
+            for b in range(PAIR_BLOCKS):
+                nc.scalar.copy(out=pair_rows_kept[:, b, :], in_=pair_rows_of[unit][b][:])
             pair_rows_kept_of[unit] = pair_rows_kept
 
         def turn_back(unit):

@@ -28,6 +28,8 @@ UNITS = BATCH * TILES
 PAIR_BLOCKS = HEADS * HEADS // P
 HEADS_PER_BLOCK = HEADS // PAIR_BLOCKS
 D_ON_GPSIMD = 5
+GPSIMD_SUMS = 1
+GPSIMD_LONE = D_ON_GPSIMD - 2 * GPSIMD_SUMS
 D_ON_VECTOR = HD - D_ON_GPSIMD
 Q_BLOCKS = Q_COLS // P
 
@@ -73,6 +75,7 @@ def tile_attention_pa_t_kernel(tc, x, w_qk, b_qk, out):
         k_of = {}
         products_of = {}
         last_products_of = {}
+        last_sums_of = {}
         pair_rows_of = {}
         pair_rows_kept_of = {}
         score_of = {}
@@ -263,24 +266,34 @@ def tile_attention_pa_t_kernel(tc, x, w_qk, b_qk, out):
             multiply(nc.gpsimd, last_products, q_kept_of[unit][:], k, D_ON_GPSIMD)
             last_products_of[unit] = last_products
 
+        def add_last_d(unit):
+            last_sums = work.tile([P, GPSIMD_SUMS, HEADS, HEADS], F32)
+            middle = GPSIMD_LONE + GPSIMD_SUMS
+            nc.gpsimd.tensor_tensor(
+                out=last_sums[:],
+                in0=last_products_of[unit][:, GPSIMD_LONE:middle, :, :],
+                in1=last_products_of[unit][:, middle:, :, :],
+                op=ALU.add,
+            )
+            last_sums_of[unit] = last_sums
+
         def sum_over_d(unit):
             pair_rows = [
                 psum_sum.tile([P, P], F32, name="pair_rows%d" % b) for b in range(PAIR_BLOCKS)
             ]
-            for d in range(HD):
-                if d < D_ON_VECTOR:
-                    of_d = products_of[unit][:, d, :, :]
-                else:
-                    of_d = last_products_of[unit][:, d - D_ON_VECTOR, :, :]
+            terms = [products_of[unit][:, d, :, :] for d in range(D_ON_VECTOR)]
+            terms += [last_products_of[unit][:, i, :, :] for i in range(GPSIMD_LONE)]
+            terms += [last_sums_of[unit][:, i, :, :] for i in range(GPSIMD_SUMS)]
+            for i, term in enumerate(terms):
                 for b in range(PAIR_BLOCKS):
                     h0 = b * HEADS_PER_BLOCK
                     nc.tensor.matmul(
                         out=pair_rows[b][:],
-                        lhsT=of_d[:, h0 : h0 + HEADS_PER_BLOCK, :].rearrange("p h g -> p (h g)"),
+                        lhsT=term[:, h0 : h0 + HEADS_PER_BLOCK, :].rearrange("p h g -> p (h g)"),
                         rhs=ident[:],
                         is_transpose=True,
-                        start=(d == 0),
-                        stop=(d == HD - 1),
+                        start=(i == 0),
+                        stop=(i == len(terms) - 1),
                     )
             pair_rows_of[unit] = pair_rows
 
@@ -359,6 +372,7 @@ def tile_attention_pa_t_kernel(tc, x, w_qk, b_qk, out):
             run_pair(add_k_bias, step - MULTIPLY_LAG)
             run_pair(quantise_x, step - QUANTISE_LAG)
             run(multiply_last_d, step - MULTIPLY_LAG)
+            run(add_last_d, step - MULTIPLY_LAG)
             run(find_low, step - SHIFT_LAG)
             run(multiply_heads, step - MULTIPLY_LAG)
             run_pair(project, step - PROJECT_LAG)

@@ -37,13 +37,14 @@ PAIR = 2
 
 LOAD_AHEAD = 4
 SORT_AHEAD = 1
-QUANTISE_LAG = PAIR
+QUANTISE_LAG = PAIR + 1
 PROJECT_LAG = QUANTISE_LAG + 1
 MULTIPLY_LAG = PROJECT_LAG + 1
 SUM_LAG = MULTIPLY_LAG + 1
 BACK_LAG = SUM_LAG + 1
 SHIFT_LAG = BACK_LAG + 1
-NORMALISE_LAG = SHIFT_LAG + 1
+INVERT_LAG = SHIFT_LAG + 1
+NORMALISE_LAG = INVERT_LAG + 1
 
 FLOPS = 2 * BATCH * TOKENS * K * QK_COLS + 2 * BATCH * TOKENS * HEADS * HEADS * HD
 
@@ -55,7 +56,7 @@ def tile_attention_pa_t_kernel(tc, x, w_qk, b_qk, out):
         const = stack.enter_context(tc.tile_pool(name="const", bufs=1))
         x_pool = stack.enter_context(tc.tile_pool(name="x_pool", bufs=LOAD_AHEAD + 1))
         work = stack.enter_context(tc.tile_pool(name="work", bufs=2))
-        soft_pool = stack.enter_context(tc.tile_pool(name="soft_pool", bufs=3))
+        soft_pool = stack.enter_context(tc.tile_pool(name="soft_pool", bufs=4))
         psum_xt = stack.enter_context(tc.psum_pool(name="psum_xt", bufs=1))
         psum_q_rows = stack.enter_context(tc.psum_pool(name="psum_q_rows", bufs=1))
         psum_k = stack.enter_context(tc.psum_pool(name="psum_k", bufs=1))
@@ -90,7 +91,8 @@ def tile_attention_pa_t_kernel(tc, x, w_qk, b_qk, out):
             nc.sync.dma_start(out=x_rows[:], in_=x[n].rearrange("(t j) k -> t j k", j=TILES)[:, j, :])
             x_rows_of[unit] = x_rows
 
-        load_x(0)
+        for unit in range(SORT_AHEAD + 1):
+            load_x(unit)
 
         ident = const.tile([P, P], F32)
         make_identity(nc, ident[:])
@@ -111,7 +113,7 @@ def tile_attention_pa_t_kernel(tc, x, w_qk, b_qk, out):
         bias = const.tile([P, QK_COLS], F32)
         q_bias = const.tile([P, Q_BLOCKS], F32)
 
-        for unit in range(1, LOAD_AHEAD):
+        for unit in range(SORT_AHEAD + 1, LOAD_AHEAD):
             load_x(unit)
 
         def prepare_weights():
@@ -368,8 +370,9 @@ def tile_attention_pa_t_kernel(tc, x, w_qk, b_qk, out):
             run(turn_q, step - MULTIPLY_LAG)
             run(keep_pair_rows, step - BACK_LAG)
             run(keep_last_q, step - MULTIPLY_LAG)
-            run(invert, step - NORMALISE_LAG)
+            run(scale_and_store, step - NORMALISE_LAG)
             run_pair(add_k_bias, step - MULTIPLY_LAG)
+            run(invert, step - INVERT_LAG)
             run_pair(quantise_x, step - QUANTISE_LAG)
             run(multiply_last_d, step - MULTIPLY_LAG)
             run(add_last_d, step - MULTIPLY_LAG)
@@ -378,12 +381,11 @@ def tile_attention_pa_t_kernel(tc, x, w_qk, b_qk, out):
             run_pair(project, step - PROJECT_LAG)
             if step == PROJECT_LAG:
                 make_q_bias()
-            run_pair(add_q_bias, step - PROJECT_LAG)
+            run(sort_x, step + SORT_AHEAD)
             run(exponential, step - SHIFT_LAG)
+            run_pair(add_q_bias, step - PROJECT_LAG)
             run(turn_x, step)
             if step == 0:
                 prepare_weights()
-            run(sort_x, step + SORT_AHEAD)
-            run(scale_and_store, step - NORMALISE_LAG)
             run(sum_over_d, step - SUM_LAG)
             run(turn_back, step - BACK_LAG)

@@ -46,6 +46,8 @@ SHIFT_LAG = BACK_LAG + 1
 INVERT_LAG = SHIFT_LAG + 1
 NORMALISE_LAG = INVERT_LAG + 1
 
+UNSORTED = MULTIPLY_LAG + 1
+
 FLOPS = 2 * BATCH * TOKENS * K * QK_COLS + 2 * BATCH * TOKENS * HEADS * HEADS * HD
 
 
@@ -91,11 +93,42 @@ def tile_attention_pa_t_kernel(tc, x, w_qk, b_qk, out):
             nc.sync.dma_start(out=x_rows[:], in_=x[n].rearrange("(t j) k -> t j k", j=TILES)[:, j, :])
             x_rows_of[unit] = x_rows
 
-        for unit in range(SORT_AHEAD + 1):
-            load_x(unit)
-
+        zero = const.tile([P, 1], F32)
+        nc.vector.memset(zero[:], 0.0)
+        one = const.tile([P, 1], F32)
+        nc.scalar.activation(out=one[:], in_=zero[:], func=ACT.Exp)
         ident = const.tile([P, P], F32)
         make_identity(nc, ident[:])
+
+        b_row = const.tile([P, QK_COLS], BF16)
+        nc.vector.memset(b_row[:], 0.0)
+        nc.sync.dma_start(out=b_row[0:1, :], in_=b_qk.rearrange("(o n) -> o n", o=1))
+        ones = const.tile([P, P], BF16)
+        nc.vector.memset(ones[:], 1.0)
+        k_bias = const.tile([P, Q_COLS], F32)
+        q_bias = const.tile([P, Q_BLOCKS], F32)
+
+        def make_biases():
+            k_bias_sum = psum_q.tile([P, Q_COLS], F32, name="q")
+            nc.tensor.matmul(
+                out=k_bias_sum[:], lhsT=ones[:], rhs=b_row[:, Q_COLS:QK_COLS], start=True, stop=True
+            )
+            nc.scalar.copy(
+                out=k_bias[:].rearrange("p (d g) -> p d g", d=HD),
+                in_=k_bias_sum[:].rearrange("p (g d) -> p d g", d=HD),
+            )
+            q_bias_sum = psum_q.tile([P, Q_BLOCKS, P], F32, name="q")
+            for b in range(Q_BLOCKS):
+                nc.tensor.matmul(
+                    out=q_bias_sum[:, b, :],
+                    lhsT=b_row[:, b * P : (b + 1) * P],
+                    rhs=ones[:],
+                    start=True,
+                    stop=True,
+                )
+            nc.scalar.activation(
+                out=q_bias[:], in_=q_bias_sum[:, :, 0], func=ACT.Copy, scale=-(HD**-0.5)
+            )
 
         w_codes = const.tile([P, PASSES, QK_COLS], U32, align_bytes=64)
         w_scales = const.tile([P, PASSES, QK_COLS], U8, align_bytes=64)
@@ -108,12 +141,8 @@ def tile_attention_pa_t_kernel(tc, x, w_qk, b_qk, out):
                 in_=w_qk[first : first + PACK * P, :].rearrange("(p v) n -> p v n", v=PACK),
             )
             w_rows_of[c] = w_rows
-        bias_bf16 = const.tile([P, QK_COLS], BF16)
-        nc.sync.dma_start(out=bias_bf16[:], in_=b_qk.partition_broadcast(P))
-        bias = const.tile([P, QK_COLS], F32)
-        q_bias = const.tile([P, Q_BLOCKS], F32)
 
-        for unit in range(SORT_AHEAD + 1, LOAD_AHEAD):
+        for unit in range(LOAD_AHEAD):
             load_x(unit)
 
         def prepare_weights():
@@ -121,23 +150,14 @@ def tile_attention_pa_t_kernel(tc, x, w_qk, b_qk, out):
                 w_grouped = const.tile(
                     [P, QK_COLS, PACK], BF16, align_bytes=64, name="w_grouped%d" % c
                 )
-                for half in range(2):
-                    cols = slice(half * Q_COLS, (half + 1) * Q_COLS)
-                    on_scalar = c == PASSES - 1 and half == 1
-                    copy = nc.scalar.copy if on_scalar else nc.vector.tensor_copy
-                    copy(
-                        out=w_grouped[:, cols, :].rearrange("p (d h) v -> p d h v", d=HD),
-                        in_=w_rows_of[c][:, :, cols].rearrange("p v (h d) -> p d h v", d=HD),
-                    )
+                nc.vector.tensor_copy(
+                    out=w_grouped[:], in_=w_rows_of[c][:].rearrange("p v n -> p n v")
+                )
                 nc.vector.quantize_mx(
                     out=w_codes[:, c, :].bitcast(FP8X4),
                     scales=w_scales[:, c, :],
                     in_=w_grouped[:].rearrange("p n v -> p (n v)"),
                 )
-            nc.scalar.copy(
-                out=bias[:].rearrange("p (c d h) -> p c d h", c=2, d=HD),
-                in_=bias_bf16[:].rearrange("p (c h d) -> p c d h", c=2, d=HD),
-            )
 
         def sort_x(unit):
             x_sorted = work.tile([P, PASSES, 2, P], F32)
@@ -151,7 +171,11 @@ def tile_attention_pa_t_kernel(tc, x, w_qk, b_qk, out):
             x_turned = psum_xt.tile([P, WORD_TILES, P], F32)
             for w in range(WORD_TILES):
                 c, u = divmod(w, 2)
-                nc.tensor.transpose(x_turned[:, w, :], x_sorted_of[unit][:, c, u, :], ident[:])
+                if unit < UNSORTED:
+                    words = x_rows_of[unit][:].bitcast(F32)[:, 2 * P * c + u : 2 * P * (c + 1) : 2]
+                else:
+                    words = x_sorted_of[unit][:, c, u, :]
+                nc.tensor.transpose(x_turned[:, w, :], words, ident[:])
             if unit % PAIR == 0:
                 x_grouped = work.tile([P, PASSES, PAIR, P * PACK], BF16, align_bytes=64)
                 x_grouped_of[unit // PAIR] = x_grouped
@@ -201,14 +225,6 @@ def tile_attention_pa_t_kernel(tc, x, w_qk, b_qk, out):
                     )
             k_sum_of[pair] = k_sum
 
-        def make_q_bias():
-            bias_rows = psum_q.tile([P, Q_BLOCKS, P], F32, name="q")
-            for b in range(Q_BLOCKS):
-                nc.tensor.transpose(bias_rows[:, b, :], bias[:, b * P : (b + 1) * P], ident[:])
-            nc.scalar.activation(
-                out=q_bias[:], in_=bias_rows[:, :, 0], func=ACT.Copy, scale=-(HD**-0.5)
-            )
-
         def add_q_bias(pair):
             q_rows = work.tile([P, Q_BLOCKS, PAIR * P], F32)
             for b in range(Q_BLOCKS):
@@ -228,19 +244,20 @@ def tile_attention_pa_t_kernel(tc, x, w_qk, b_qk, out):
                 nc.tensor.transpose(
                     q[:, b * P : (b + 1) * P], q_rows_of[unit // PAIR][:, b, tokens], ident[:]
                 )
-            q_of[unit] = q
+            q_of[unit] = q[:].rearrange("p (h d) -> p d h", d=HD)
 
         def keep_last_q(unit):
-            q_kept = work.tile([P, D_ON_GPSIMD * HEADS], F32)
-            nc.scalar.copy(out=q_kept[:], in_=q_of[unit][:, D_ON_VECTOR * HEADS :])
+            q_kept = work.tile([P, D_ON_GPSIMD, HEADS], F32)
+            nc.scalar.copy(out=q_kept[:], in_=q_of[unit][:, D_ON_VECTOR:, :])
             q_kept_of[unit] = q_kept
 
         def add_k_bias(pair):
-            k = work.tile([P, PAIR, Q_COLS], F32)
+            k = work.tile([P, PAIR, HD, HEADS], F32)
+            for_each = k_bias[:].rearrange("p (d g) -> p d g", d=HD).unsqueeze(1)
             nc.vector.tensor_tensor(
                 out=k[:],
-                in0=k_sum_of[pair][:],
-                in1=bias[:, Q_COLS:QK_COLS].unsqueeze(1).to_broadcast([P, PAIR, Q_COLS]),
+                in0=k_sum_of[pair][:].rearrange("p j (g d) -> p j d g", d=HD),
+                in1=for_each.to_broadcast([P, PAIR, HD, HEADS]),
                 op=ALU.add,
             )
             k_of[pair] = k
@@ -249,22 +266,20 @@ def tile_attention_pa_t_kernel(tc, x, w_qk, b_qk, out):
             shape = [P, count, HEADS, HEADS]
             engine.tensor_tensor(
                 out=products[:],
-                in0=q.rearrange("p (d h) -> p d h", d=count).unsqueeze(3).to_broadcast(shape),
-                in1=k.rearrange("p (d g) -> p d g", d=count).unsqueeze(2).to_broadcast(shape),
+                in0=q.unsqueeze(3).to_broadcast(shape),
+                in1=k.unsqueeze(2).to_broadcast(shape),
                 op=ALU.mult,
             )
 
         def multiply_heads(unit):
             products = work.tile([P, D_ON_VECTOR, HEADS, HEADS], F32)
-            cols = slice(0, D_ON_VECTOR * HEADS)
-            k = k_of[unit // PAIR][:, unit % PAIR, cols]
-            multiply(nc.vector, products, q_of[unit][:, cols], k, D_ON_VECTOR)
+            k = k_of[unit // PAIR][:, unit % PAIR, :D_ON_VECTOR, :]
+            multiply(nc.vector, products, q_of[unit][:, :D_ON_VECTOR, :], k, D_ON_VECTOR)
             products_of[unit] = products
 
         def multiply_last_d(unit):
             last_products = work.tile([P, D_ON_GPSIMD, HEADS, HEADS], F32)
-            cols = slice(D_ON_VECTOR * HEADS, Q_COLS)
-            k = k_of[unit // PAIR][:, unit % PAIR, cols]
+            k = k_of[unit // PAIR][:, unit % PAIR, D_ON_VECTOR:, :]
             multiply(nc.gpsimd, last_products, q_kept_of[unit][:], k, D_ON_GPSIMD)
             last_products_of[unit] = last_products
 
@@ -364,7 +379,7 @@ def tile_attention_pa_t_kernel(tc, x, w_qk, b_qk, out):
             if 0 <= unit < UNITS and unit % PAIR == 0:
                 stage(unit // PAIR)
 
-        sort_x(0)
+        make_biases()
         for step in range(UNITS + NORMALISE_LAG):
             run(load_x, step + LOAD_AHEAD)
             run(turn_q, step - MULTIPLY_LAG)
@@ -379,9 +394,8 @@ def tile_attention_pa_t_kernel(tc, x, w_qk, b_qk, out):
             run(find_low, step - SHIFT_LAG)
             run(multiply_heads, step - MULTIPLY_LAG)
             run_pair(project, step - PROJECT_LAG)
-            if step == PROJECT_LAG:
-                make_q_bias()
-            run(sort_x, step + SORT_AHEAD)
+            if step + SORT_AHEAD >= UNSORTED:
+                run(sort_x, step + SORT_AHEAD)
             run(exponential, step - SHIFT_LAG)
             run_pair(add_q_bias, step - PROJECT_LAG)
             run(turn_x, step)

@@ -27,6 +27,8 @@ TILES = TOKENS // P
 UNITS = BATCH * TILES
 PAIR_BLOCKS = HEADS * HEADS // P
 HEADS_PER_BLOCK = HEADS // PAIR_BLOCKS
+ALL_BLOCKS = tuple(range(PAIR_BLOCKS))
+BLOCK_BY_BLOCK = [(b,) for b in ALL_BLOCKS]
 D_ON_GPSIMD = 5
 GPSIMD_SUMS = 1
 GPSIMD_LONE = D_ON_GPSIMD - 2 * GPSIMD_SUMS
@@ -45,6 +47,7 @@ BACK_LAG = SUM_LAG + 1
 SHIFT_LAG = BACK_LAG + 1
 INVERT_LAG = SHIFT_LAG + 1
 NORMALISE_LAG = INVERT_LAG + 1
+LAST_ON_VECTOR = INVERT_LAG - MULTIPLY_LAG
 
 UNSORTED = MULTIPLY_LAG + 1
 
@@ -134,6 +137,7 @@ def tile_attention_pa_t_kernel(tc, x, w_qk, b_qk, out):
         w_scales = const.tile([P, PASSES, QK_COLS], U8, align_bytes=64)
         w_rows_of = {}
         for c in range(PASSES):
+            load_x(c)
             w_rows = const.tile([P, PACK, QK_COLS], BF16, name="w_rows%d" % c)
             first = c * PACK * P
             nc.sync.dma_start(
@@ -142,7 +146,7 @@ def tile_attention_pa_t_kernel(tc, x, w_qk, b_qk, out):
             )
             w_rows_of[c] = w_rows
 
-        for unit in range(LOAD_AHEAD):
+        for unit in range(PASSES, LOAD_AHEAD):
             load_x(unit)
 
         def prepare_weights():
@@ -168,7 +172,8 @@ def tile_attention_pa_t_kernel(tc, x, w_qk, b_qk, out):
             x_sorted_of[unit] = x_sorted
 
         def turn_x(unit):
-            x_turned = psum_xt.tile([P, WORD_TILES, P], F32)
+            pool, name = (psum_back, "score") if unit < UNSORTED and unit % 2 else (psum_xt, "x_turned")
+            x_turned = pool.tile([P, WORD_TILES, P], F32, name=name)
             for w in range(WORD_TILES):
                 c, u = divmod(w, 2)
                 if unit < UNSORTED:
@@ -262,8 +267,11 @@ def tile_attention_pa_t_kernel(tc, x, w_qk, b_qk, out):
             )
             k_of[pair] = k
 
-        def multiply(engine, products, q, k, count):
-            shape = [P, count, HEADS, HEADS]
+        def heads_of(blocks):
+            return slice(blocks[0] * HEADS_PER_BLOCK, (blocks[-1] + 1) * HEADS_PER_BLOCK)
+
+        def multiply(engine, products, q, k):
+            shape = products[:].shape
             engine.tensor_tensor(
                 out=products[:],
                 in0=q.unsqueeze(3).to_broadcast(shape),
@@ -271,39 +279,48 @@ def tile_attention_pa_t_kernel(tc, x, w_qk, b_qk, out):
                 op=ALU.mult,
             )
 
-        def multiply_heads(unit):
-            products = work.tile([P, D_ON_VECTOR, HEADS, HEADS], F32)
-            k = k_of[unit // PAIR][:, unit % PAIR, :D_ON_VECTOR, :]
-            multiply(nc.vector, products, q_of[unit][:, :D_ON_VECTOR, :], k, D_ON_VECTOR)
-            products_of[unit] = products
+        def multiply_heads(unit, blocks):
+            heads = heads_of(blocks)
+            products = work.tile(
+                [P, D_ON_VECTOR, heads.stop - heads.start, HEADS], F32, name="products" + tag(blocks)
+            )
+            q = q_of[unit][:, :D_ON_VECTOR, heads]
+            multiply(nc.vector, products, q, k_of[unit // PAIR][:, unit % PAIR, :D_ON_VECTOR, :])
+            products_of[unit, blocks] = products
 
-        def multiply_last_d(unit):
-            last_products = work.tile([P, D_ON_GPSIMD, HEADS, HEADS], F32)
-            k = k_of[unit // PAIR][:, unit % PAIR, D_ON_VECTOR:, :]
-            multiply(nc.gpsimd, last_products, q_kept_of[unit][:], k, D_ON_GPSIMD)
-            last_products_of[unit] = last_products
+        def multiply_last_d(unit, blocks):
+            heads = heads_of(blocks)
+            last_products = work.tile(
+                [P, D_ON_GPSIMD, heads.stop - heads.start, HEADS], F32, name="last" + tag(blocks)
+            )
+            q = q_kept_of[unit][:, :, heads]
+            multiply(nc.gpsimd, last_products, q, k_of[unit // PAIR][:, unit % PAIR, D_ON_VECTOR:, :])
+            last_products_of[unit, blocks] = last_products
 
-        def add_last_d(unit):
+        def add_last_d(unit, blocks):
+            if blocks != ALL_BLOCKS:
+                return
             last_sums = work.tile([P, GPSIMD_SUMS, HEADS, HEADS], F32)
             middle = GPSIMD_LONE + GPSIMD_SUMS
+            last_products = last_products_of[unit, blocks]
             nc.gpsimd.tensor_tensor(
                 out=last_sums[:],
-                in0=last_products_of[unit][:, GPSIMD_LONE:middle, :, :],
-                in1=last_products_of[unit][:, middle:, :, :],
+                in0=last_products[:, GPSIMD_LONE:middle, :, :],
+                in1=last_products[:, middle:, :, :],
                 op=ALU.add,
             )
-            last_sums_of[unit] = last_sums
+            last_sums_of[unit, blocks] = last_sums
 
-        def sum_over_d(unit):
-            pair_rows = [
-                psum_sum.tile([P, P], F32, name="pair_rows%d" % b) for b in range(PAIR_BLOCKS)
-            ]
-            terms = [products_of[unit][:, d, :, :] for d in range(D_ON_VECTOR)]
-            terms += [last_products_of[unit][:, i, :, :] for i in range(GPSIMD_LONE)]
-            terms += [last_sums_of[unit][:, i, :, :] for i in range(GPSIMD_SUMS)]
+        def sum_over_d(unit, blocks):
+            pair_rows = {b: psum_sum.tile([P, P], F32, name="pair_rows%d" % b) for b in blocks}
+            lone = GPSIMD_LONE if blocks == ALL_BLOCKS else D_ON_GPSIMD
+            terms = [products_of[unit, blocks][:, d, :, :] for d in range(D_ON_VECTOR)]
+            terms += [last_products_of[unit, blocks][:, i, :, :] for i in range(lone)]
+            if blocks == ALL_BLOCKS:
+                terms += [last_sums_of[unit, blocks][:, i, :, :] for i in range(GPSIMD_SUMS)]
             for i, term in enumerate(terms):
-                for b in range(PAIR_BLOCKS):
-                    h0 = b * HEADS_PER_BLOCK
+                for j, b in enumerate(blocks):
+                    h0 = j * HEADS_PER_BLOCK
                     nc.tensor.matmul(
                         out=pair_rows[b][:],
                         lhsT=term[:, h0 : h0 + HEADS_PER_BLOCK, :].rearrange("p h g -> p (h g)"),
@@ -312,68 +329,104 @@ def tile_attention_pa_t_kernel(tc, x, w_qk, b_qk, out):
                         start=(i == 0),
                         stop=(i == len(terms) - 1),
                     )
-            pair_rows_of[unit] = pair_rows
+            pair_rows_of[unit, blocks] = pair_rows
 
-        def keep_pair_rows(unit):
-            pair_rows_kept = work.tile([P, PAIR_BLOCKS, P], F32)
-            for b in range(PAIR_BLOCKS):
-                nc.scalar.copy(out=pair_rows_kept[:, b, :], in_=pair_rows_of[unit][b][:])
-            pair_rows_kept_of[unit] = pair_rows_kept
+        def keep_pair_rows(unit, blocks):
+            pair_rows_kept = work.tile([P, len(blocks), P], F32, name="kept" + tag(blocks))
+            copy = nc.scalar.copy if blocks == ALL_BLOCKS else nc.vector.tensor_copy
+            for j, b in enumerate(blocks):
+                copy(out=pair_rows_kept[:, j, :], in_=pair_rows_of[unit, blocks][b][:])
+            pair_rows_kept_of[unit, blocks] = pair_rows_kept
 
-        def turn_back(unit):
-            score = psum_back.tile([P, HEADS, HEADS], F32)
-            for b in range(PAIR_BLOCKS):
-                h0 = b * HEADS_PER_BLOCK
+        def turn_back(unit, blocks):
+            pool, name = {
+                ALL_BLOCKS: (psum_back, "score"),
+                BLOCK_BY_BLOCK[0]: (psum_xt, "x_turned"),
+                BLOCK_BY_BLOCK[1]: (psum_k, "k_sum"),
+            }[blocks]
+            heads = heads_of(blocks)
+            score = pool.tile([P, heads.stop - heads.start, HEADS], F32, name=name)
+            for j in range(len(blocks)):
+                h0 = j * HEADS_PER_BLOCK
                 nc.tensor.transpose(
                     score[:, h0 : h0 + HEADS_PER_BLOCK, :].rearrange("p h g -> p (h g)"),
-                    pair_rows_kept_of[unit][:, b, :],
+                    pair_rows_kept_of[unit, blocks][:, j, :],
                     ident[:],
                 )
-            score_of[unit] = score
+            score_of[unit, blocks] = score
 
-        def find_low(unit):
-            low = soft_pool.tile([P, HEADS], F32)
-            nc.vector.tensor_reduce(out=low[:], in_=score_of[unit][:], axis=AXIS.X, op=ALU.min)
-            low_of[unit] = low
+        def find_low(unit, blocks):
+            heads = heads_of(blocks)
+            low = soft_pool.tile([P, heads.stop - heads.start], F32, name="low" + tag(blocks))
+            nc.vector.tensor_reduce(
+                out=low[:], in_=score_of[unit, blocks][:], axis=AXIS.X, op=ALU.min
+            )
+            low_of[unit, blocks] = low
 
-        def exponential(unit):
-            prob = soft_pool.tile([P, HEADS, HEADS], F32)
-            total = soft_pool.tile([P, HEADS], F32)
-            for h in range(HEADS):
+        def exponential(unit, blocks):
+            heads = heads_of(blocks)
+            count = heads.stop - heads.start
+            prob = soft_pool.tile([P, count, HEADS], F32, name="prob" + tag(blocks))
+            total = soft_pool.tile([P, count], F32, name="total" + tag(blocks))
+            for h in range(count):
                 nc.scalar.activation(
                     out=prob[:, h, :],
-                    in_=score_of[unit][:, h, :],
+                    in_=score_of[unit, blocks][:, h, :],
                     func=ACT.Exp,
-                    bias=low_of[unit][:, h : h + 1],
+                    bias=low_of[unit, blocks][:, h : h + 1],
                     scale=-1.0,
                     accum_out=total[:, h : h + 1],
                 )
-            prob_of[unit] = prob
-            total_of[unit] = total
+            prob_of[unit, blocks] = prob
+            total_of[unit, blocks] = total
 
-        def invert(unit):
-            inverse = soft_pool.tile([P, HEADS], F32)
-            nc.vector.reciprocal(out=inverse[:], in_=total_of[unit][:])
-            inverse_of[unit] = inverse
+        def invert(unit, blocks):
+            heads = heads_of(blocks)
+            total = total_of[unit, blocks]
+            inverse = soft_pool.tile([P, heads.stop - heads.start], F32, name="inverse" + tag(blocks))
+            nc.vector.reciprocal(out=inverse[:], in_=total[:])
+            inverse_of[unit, blocks] = inverse
+            if unit >= UNITS - LAST_ON_VECTOR:
+                prob = prob_of[unit, blocks]
+                nc.vector.tensor_tensor(
+                    out=prob[:],
+                    in0=prob[:],
+                    in1=inverse[:].unsqueeze(2).to_broadcast(prob[:].shape),
+                    op=ALU.mult,
+                )
+                store(unit, blocks)
 
-        def scale_and_store(unit):
-            n, j = divmod(unit, TILES)
-            prob = prob_of[unit]
+        def scale_and_store(unit, blocks):
+            if unit >= UNITS - LAST_ON_VECTOR:
+                return
+            prob = prob_of[unit, blocks]
             for h in range(HEADS):
                 nc.scalar.activation(
                     out=prob[:, h, :],
                     in_=prob[:, h, :],
                     func=ACT.Copy,
-                    scale=inverse_of[unit][:, h : h + 1],
+                    scale=inverse_of[unit, blocks][:, h : h + 1],
                 )
+            store(unit, blocks)
+
+        def store(unit, blocks):
+            n, j = divmod(unit, TILES)
             nc.sync.dma_start(
-                out=out[n].rearrange("(t j) h g -> t j (h g)", j=TILES)[:, j, :],
-                in_=prob[:].rearrange("p h g -> p (h g)"),
+                out=out[n].rearrange("(t j) h g -> t j h g", j=TILES)[:, j, heads_of(blocks), :],
+                in_=prob_of[unit, blocks][:],
             )
+
+        def tag(blocks):
+            return "" if blocks == ALL_BLOCKS else "_of_block"
 
         def run(stage, unit):
             if 0 <= unit < UNITS:
                 stage(unit)
+
+        def run_blocks(stage, unit):
+            if 0 <= unit < UNITS:
+                for blocks in BLOCK_BY_BLOCK if unit == UNITS - 1 else [ALL_BLOCKS]:
+                    stage(unit, blocks)
 
         def run_pair(stage, unit):
             if 0 <= unit < UNITS and unit % PAIR == 0:
@@ -383,23 +436,23 @@ def tile_attention_pa_t_kernel(tc, x, w_qk, b_qk, out):
         for step in range(UNITS + NORMALISE_LAG):
             run(load_x, step + LOAD_AHEAD)
             run(turn_q, step - MULTIPLY_LAG)
-            run(keep_pair_rows, step - BACK_LAG)
+            run_blocks(keep_pair_rows, step - BACK_LAG)
             run(keep_last_q, step - MULTIPLY_LAG)
-            run(scale_and_store, step - NORMALISE_LAG)
+            run_blocks(scale_and_store, step - NORMALISE_LAG)
             run_pair(add_k_bias, step - MULTIPLY_LAG)
-            run(invert, step - INVERT_LAG)
+            run_blocks(invert, step - INVERT_LAG)
             run_pair(quantise_x, step - QUANTISE_LAG)
-            run(multiply_last_d, step - MULTIPLY_LAG)
-            run(add_last_d, step - MULTIPLY_LAG)
-            run(find_low, step - SHIFT_LAG)
-            run(multiply_heads, step - MULTIPLY_LAG)
+            run_blocks(multiply_last_d, step - MULTIPLY_LAG)
+            run_blocks(add_last_d, step - MULTIPLY_LAG)
+            run_blocks(find_low, step - SHIFT_LAG)
+            run_blocks(multiply_heads, step - MULTIPLY_LAG)
             run_pair(project, step - PROJECT_LAG)
             if step + SORT_AHEAD >= UNSORTED:
                 run(sort_x, step + SORT_AHEAD)
-            run(exponential, step - SHIFT_LAG)
+            run_blocks(exponential, step - SHIFT_LAG)
             run_pair(add_q_bias, step - PROJECT_LAG)
             run(turn_x, step)
             if step == 0:
                 prepare_weights()
-            run(sum_over_d, step - SUM_LAG)
-            run(turn_back, step - BACK_LAG)
+            run_blocks(sum_over_d, step - SUM_LAG)
+            run_blocks(turn_back, step - BACK_LAG)

@@ -29,9 +29,7 @@ PAIR_BLOCKS = HEADS * HEADS // P
 HEADS_PER_BLOCK = HEADS // PAIR_BLOCKS
 ALL_BLOCKS = tuple(range(PAIR_BLOCKS))
 BLOCK_BY_BLOCK = [(b,) for b in ALL_BLOCKS]
-D_ON_GPSIMD = 5
-GPSIMD_SUMS = 1
-GPSIMD_LONE = D_ON_GPSIMD - 2 * GPSIMD_SUMS
+D_ON_GPSIMD = 6
 D_ON_VECTOR = HD - D_ON_GPSIMD
 Q_BLOCKS = Q_COLS // P
 
@@ -81,7 +79,6 @@ def tile_attention_pa_t_kernel(tc, x, w_qk, b_qk, out):
         k_of = {}
         products_of = {}
         last_products_of = {}
-        last_sums_of = {}
         pair_rows_of = {}
         pair_rows_kept_of = {}
         score_of = {}
@@ -297,27 +294,10 @@ def tile_attention_pa_t_kernel(tc, x, w_qk, b_qk, out):
             multiply(nc.gpsimd, last_products, q, k_of[unit // PAIR][:, unit % PAIR, D_ON_VECTOR:, :])
             last_products_of[unit, blocks] = last_products
 
-        def add_last_d(unit, blocks):
-            if blocks != ALL_BLOCKS:
-                return
-            last_sums = work.tile([P, GPSIMD_SUMS, HEADS, HEADS], F32)
-            middle = GPSIMD_LONE + GPSIMD_SUMS
-            last_products = last_products_of[unit, blocks]
-            nc.gpsimd.tensor_tensor(
-                out=last_sums[:],
-                in0=last_products[:, GPSIMD_LONE:middle, :, :],
-                in1=last_products[:, middle:, :, :],
-                op=ALU.add,
-            )
-            last_sums_of[unit, blocks] = last_sums
-
         def sum_over_d(unit, blocks):
             pair_rows = {b: psum_sum.tile([P, P], F32, name="pair_rows%d" % b) for b in blocks}
-            lone = GPSIMD_LONE if blocks == ALL_BLOCKS else D_ON_GPSIMD
             terms = [products_of[unit, blocks][:, d, :, :] for d in range(D_ON_VECTOR)]
-            terms += [last_products_of[unit, blocks][:, i, :, :] for i in range(lone)]
-            if blocks == ALL_BLOCKS:
-                terms += [last_sums_of[unit, blocks][:, i, :, :] for i in range(GPSIMD_SUMS)]
+            terms += [last_products_of[unit, blocks][:, i, :, :] for i in range(D_ON_GPSIMD)]
             for i, term in enumerate(terms):
                 for j, b in enumerate(blocks):
                     h0 = j * HEADS_PER_BLOCK
@@ -443,7 +423,6 @@ def tile_attention_pa_t_kernel(tc, x, w_qk, b_qk, out):
             run_blocks(invert, step - INVERT_LAG)
             run_pair(quantise_x, step - QUANTISE_LAG)
             run_blocks(multiply_last_d, step - MULTIPLY_LAG)
-            run_blocks(add_last_d, step - MULTIPLY_LAG)
             run_blocks(find_low, step - SHIFT_LAG)
             run_blocks(multiply_heads, step - MULTIPLY_LAG)
             run_pair(project, step - PROJECT_LAG)

@@ -60,12 +60,9 @@ def tile_attention_pa_t_kernel(tc, x, w_qk, b_qk, out):
         x_pool = stack.enter_context(tc.tile_pool(name="x_pool", bufs=LOAD_AHEAD + 1))
         work = stack.enter_context(tc.tile_pool(name="work", bufs=2))
         soft_pool = stack.enter_context(tc.tile_pool(name="soft_pool", bufs=4))
-        psum_xt = stack.enter_context(tc.psum_pool(name="psum_xt", bufs=1))
-        psum_q_rows = stack.enter_context(tc.psum_pool(name="psum_q_rows", bufs=1))
-        psum_k = stack.enter_context(tc.psum_pool(name="psum_k", bufs=1))
+        psum_turns = stack.enter_context(tc.psum_pool(name="psum_turns", bufs=4))
         psum_q = stack.enter_context(tc.psum_pool(name="psum_q", bufs=2))
         psum_sum = stack.enter_context(tc.psum_pool(name="psum_sum", bufs=1))
-        psum_back = stack.enter_context(tc.psum_pool(name="psum_back", bufs=1))
 
         x_rows_of = {}
         x_sorted_of = {}
@@ -169,8 +166,7 @@ def tile_attention_pa_t_kernel(tc, x, w_qk, b_qk, out):
             x_sorted_of[unit] = x_sorted
 
         def turn_x(unit):
-            pool, name = (psum_back, "score") if unit < UNSORTED and unit % 2 else (psum_xt, "x_turned")
-            x_turned = pool.tile([P, WORD_TILES, P], F32, name=name)
+            x_turned = psum_turns.tile([P, WORD_TILES, P], F32, name="turn")
             for w in range(WORD_TILES):
                 c, u = divmod(w, 2)
                 if unit < UNSORTED:
@@ -200,7 +196,7 @@ def tile_attention_pa_t_kernel(tc, x, w_qk, b_qk, out):
 
         def project(pair):
             x_codes, x_scales = x_mx_of[pair]
-            q_rows_sum = psum_q_rows.tile([P, Q_BLOCKS, PAIR * P], F32)
+            q_rows_sum = psum_turns.tile([P, Q_BLOCKS, PAIR * P], F32, name="turn")
             for b in range(Q_BLOCKS):
                 for c in range(PASSES):
                     nc.tensor.matmul_mx(
@@ -213,7 +209,7 @@ def tile_attention_pa_t_kernel(tc, x, w_qk, b_qk, out):
                         stop=(c == PASSES - 1),
                     )
             q_rows_sum_of[pair] = q_rows_sum
-            k_sum = psum_k.tile([P, PAIR, Q_COLS], F32)
+            k_sum = psum_turns.tile([P, PAIR, Q_COLS], F32, name="turn")
             for j in range(PAIR):
                 for c in range(PASSES):
                     nc.tensor.matmul_mx(
@@ -319,13 +315,8 @@ def tile_attention_pa_t_kernel(tc, x, w_qk, b_qk, out):
             pair_rows_kept_of[unit, blocks] = pair_rows_kept
 
         def turn_back(unit, blocks):
-            pool, name = {
-                ALL_BLOCKS: (psum_back, "score"),
-                BLOCK_BY_BLOCK[0]: (psum_xt, "x_turned"),
-                BLOCK_BY_BLOCK[1]: (psum_k, "k_sum"),
-            }[blocks]
             heads = heads_of(blocks)
-            score = pool.tile([P, heads.stop - heads.start, HEADS], F32, name=name)
+            score = psum_turns.tile([P, heads.stop - heads.start, HEADS], F32, name="turn")
             for j in range(len(blocks)):
                 h0 = j * HEADS_PER_BLOCK
                 nc.tensor.transpose(

@@ -60,9 +60,8 @@ def tile_attention_pa_t_kernel(tc, x, w_qk, b_qk, out):
         x_pool = stack.enter_context(tc.tile_pool(name="x_pool", bufs=LOAD_AHEAD + 1))
         work = stack.enter_context(tc.tile_pool(name="work", bufs=2))
         soft_pool = stack.enter_context(tc.tile_pool(name="soft_pool", bufs=4))
-        psum_turns = stack.enter_context(tc.psum_pool(name="psum_turns", bufs=4))
+        psum_turns = stack.enter_context(tc.psum_pool(name="psum_turns", bufs=6))
         psum_q = stack.enter_context(tc.psum_pool(name="psum_q", bufs=2))
-        psum_sum = stack.enter_context(tc.psum_pool(name="psum_sum", bufs=1))
 
         x_rows_of = {}
         x_sorted_of = {}
@@ -291,7 +290,7 @@ def tile_attention_pa_t_kernel(tc, x, w_qk, b_qk, out):
             last_products_of[unit, blocks] = last_products
 
         def sum_over_d(unit, blocks):
-            pair_rows = {b: psum_sum.tile([P, P], F32, name="pair_rows%d" % b) for b in blocks}
+            pair_rows = {b: psum_turns.tile([P, P], F32, name="turn") for b in blocks}
             terms = [products_of[unit, blocks][:, d, :, :] for d in range(D_ON_VECTOR)]
             terms += [last_products_of[unit, blocks][:, i, :, :] for i in range(D_ON_GPSIMD)]
             for i, term in enumerate(terms):

@@ -44,8 +44,8 @@ SUM_LAG = MULTIPLY_LAG + 1
 BACK_LAG = SUM_LAG + 1
 SHIFT_LAG = BACK_LAG + 1
 INVERT_LAG = SHIFT_LAG + 1
-NORMALISE_LAG = INVERT_LAG + 1
-LAST_ON_VECTOR = INVERT_LAG - MULTIPLY_LAG
+NORMALISE_LAG = INVERT_LAG + PAIR
+LAST_SCALED = UNITS - (INVERT_LAG - MULTIPLY_LAG)
 
 UNSORTED = MULTIPLY_LAG + 1
 
@@ -59,7 +59,7 @@ def tile_attention_pa_t_kernel(tc, x, w_qk, b_qk, out):
         const = stack.enter_context(tc.tile_pool(name="const", bufs=1))
         x_pool = stack.enter_context(tc.tile_pool(name="x_pool", bufs=LOAD_AHEAD + 1))
         work = stack.enter_context(tc.tile_pool(name="work", bufs=2))
-        soft_pool = stack.enter_context(tc.tile_pool(name="soft_pool", bufs=4))
+        soft_pool = stack.enter_context(tc.tile_pool(name="soft_pool", bufs=5))
         psum_turns = stack.enter_context(tc.psum_pool(name="psum_turns", bufs=6))
         psum_q = stack.enter_context(tc.psum_pool(name="psum_q", bufs=2))
 
@@ -81,6 +81,7 @@ def tile_attention_pa_t_kernel(tc, x, w_qk, b_qk, out):
         low_of = {}
         prob_of = {}
         total_of = {}
+        totals_of = {}
         inverse_of = {}
 
         def load_x(unit):
@@ -130,7 +131,6 @@ def tile_attention_pa_t_kernel(tc, x, w_qk, b_qk, out):
         w_scales = const.tile([P, PASSES, QK_COLS], U8, align_bytes=64)
         w_rows_of = {}
         for c in range(PASSES):
-            load_x(c)
             w_rows = const.tile([P, PACK, QK_COLS], BF16, name="w_rows%d" % c)
             first = c * PACK * P
             nc.sync.dma_start(
@@ -138,6 +138,7 @@ def tile_attention_pa_t_kernel(tc, x, w_qk, b_qk, out):
                 in_=w_qk[first : first + PACK * P, :].rearrange("(p v) n -> p v n", v=PACK),
             )
             w_rows_of[c] = w_rows
+            load_x(c)
 
         for unit in range(PASSES, LOAD_AHEAD):
             load_x(unit)
@@ -337,7 +338,12 @@ def tile_attention_pa_t_kernel(tc, x, w_qk, b_qk, out):
             heads = heads_of(blocks)
             count = heads.stop - heads.start
             prob = soft_pool.tile([P, count, HEADS], F32, name="prob" + tag(blocks))
-            total = soft_pool.tile([P, count], F32, name="total" + tag(blocks))
+            if unit >= LAST_SCALED:
+                total = soft_pool.tile([P, count], F32, name="total" + tag(blocks))
+            else:
+                if unit % PAIR == 0:
+                    totals_of[unit // PAIR] = soft_pool.tile([P, PAIR, count], F32, name="totals")
+                total = totals_of[unit // PAIR][:, unit % PAIR, :]
             for h in range(count):
                 nc.scalar.activation(
                     out=prob[:, h, :],
@@ -352,22 +358,26 @@ def tile_attention_pa_t_kernel(tc, x, w_qk, b_qk, out):
 
         def invert(unit, blocks):
             heads = heads_of(blocks)
-            total = total_of[unit, blocks]
+            if unit < LAST_SCALED:
+                if unit % PAIR == PAIR - 1:
+                    inverses = soft_pool.tile([P, PAIR, HEADS], F32)
+                    nc.vector.reciprocal(out=inverses[:], in_=totals_of[unit // PAIR][:])
+                    for j in range(PAIR):
+                        inverse_of[unit - unit % PAIR + j] = inverses[:, j, :]
+                return
             inverse = soft_pool.tile([P, heads.stop - heads.start], F32, name="inverse" + tag(blocks))
-            nc.vector.reciprocal(out=inverse[:], in_=total[:])
-            inverse_of[unit, blocks] = inverse
-            if unit >= UNITS - LAST_ON_VECTOR:
-                prob = prob_of[unit, blocks]
-                nc.vector.tensor_tensor(
-                    out=prob[:],
-                    in0=prob[:],
-                    in1=inverse[:].unsqueeze(2).to_broadcast(prob[:].shape),
-                    op=ALU.mult,
-                )
-                store(unit, blocks)
+            nc.vector.reciprocal(out=inverse[:], in_=total_of[unit, blocks][:])
+            prob = prob_of[unit, blocks]
+            nc.vector.tensor_tensor(
+                out=prob[:],
+                in0=prob[:],
+                in1=inverse[:].unsqueeze(2).to_broadcast(prob[:].shape),
+                op=ALU.mult,
+            )
+            store(unit, blocks)
 
         def scale_and_store(unit, blocks):
-            if unit >= UNITS - LAST_ON_VECTOR:
+            if unit >= LAST_SCALED:
                 return
             prob = prob_of[unit, blocks]
             for h in range(HEADS):
@@ -375,7 +385,7 @@ def tile_attention_pa_t_kernel(tc, x, w_qk, b_qk, out):
                     out=prob[:, h, :],
                     in_=prob[:, h, :],
                     func=ACT.Copy,
-                    scale=inverse_of[unit, blocks][:, h : h + 1],
+                    scale=inverse_of[unit][:, h : h + 1],
                 )
             store(unit, blocks)
 
@@ -410,8 +420,8 @@ def tile_attention_pa_t_kernel(tc, x, w_qk, b_qk, out):
             run(keep_last_q, step - MULTIPLY_LAG)
             run_blocks(scale_and_store, step - NORMALISE_LAG)
             run_pair(add_k_bias, step - MULTIPLY_LAG)
-            run_blocks(invert, step - INVERT_LAG)
             run_pair(quantise_x, step - QUANTISE_LAG)
+            run_blocks(invert, step - INVERT_LAG)
             run_blocks(multiply_last_d, step - MULTIPLY_LAG)
             run_blocks(find_low, step - SHIFT_LAG)
             run_blocks(multiply_heads, step - MULTIPLY_LAG)

from contextlib import ExitStack

import concourse.mybir as mybir
from concourse.masks import make_identity

F32 = mybir.dt.float32
BF16 = mybir.dt.bfloat16
U32 = mybir.dt.uint32
U8 = mybir.dt.uint8
FP8X4 = mybir.dt.float8_e4m3fn_x4
ALU = mybir.AluOpType
ACT = mybir.ActivationFunctionType
AXIS = mybir.AxisListType

P = 128
BATCH = 8
TOKENS = 1024
K = 1024
HEADS = 16
HD = 16
Q_COLS = HEADS * HD
QK_COLS = 2 * Q_COLS
PACK = 4
PASSES = K // (P * PACK)
WORD_TILES = K // 2 // P
TILES = TOKENS // P
UNITS = BATCH * TILES
PAIR_BLOCKS = HEADS * HEADS // P
HEADS_PER_BLOCK = HEADS // PAIR_BLOCKS
ALL_BLOCKS = tuple(range(PAIR_BLOCKS))
BLOCK_BY_BLOCK = [(b,) for b in ALL_BLOCKS]
D_ON_GPSIMD = 6
D_ON_VECTOR = HD - D_ON_GPSIMD
Q_BLOCKS = Q_COLS // P

PAIR = 2

LOAD_AHEAD = 4
SORT_AHEAD = 1
QUANTISE_LAG = PAIR + 1
PROJECT_LAG = QUANTISE_LAG + 1
MULTIPLY_LAG = PROJECT_LAG + 1
SUM_LAG = MULTIPLY_LAG + 1
BACK_LAG = SUM_LAG + 1
SHIFT_LAG = BACK_LAG + 1
INVERT_LAG = SHIFT_LAG + 1
NORMALISE_LAG = INVERT_LAG + PAIR
LAST_SCALED = UNITS - (INVERT_LAG - MULTIPLY_LAG)

UNSORTED = MULTIPLY_LAG + 1

FLOPS = 2 * BATCH * TOKENS * K * QK_COLS + 2 * BATCH * TOKENS * HEADS * HEADS * HD


def tile_attention_pa_t_kernel(tc, x, w_qk, b_qk, out):
    nc = tc.nc
    with ExitStack() as stack:
        stack.enter_context(tc.manual_schedule())
        const = stack.enter_context(tc.tile_pool(name="const", bufs=1))
        x_pool = stack.enter_context(tc.tile_pool(name="x_pool", bufs=LOAD_AHEAD + 1))
        work = stack.enter_context(tc.tile_pool(name="work", bufs=2))
        soft_pool = stack.enter_context(tc.tile_pool(name="soft_pool", bufs=5))
        psum_turns = stack.enter_context(tc.psum_pool(name="psum_turns", bufs=6))
        psum_q = stack.enter_context(tc.psum_pool(name="psum_q", bufs=2))

        x_rows_of = {}
        x_sorted_of = {}
        x_grouped_of = {}
        x_mx_of = {}
        q_rows_sum_of = {}
        q_rows_of = {}
        q_of = {}
        q_kept_of = {}
        k_sum_of = {}
        k_of = {}
        products_of = {}
        last_products_of = {}
        pair_rows_of = {}
        pair_rows_kept_of = {}
        score_of = {}
        low_of = {}
        prob_of = {}
        total_of = {}
        totals_of = {}
        inverse_of = {}

        def load_x(unit):
            n, j = divmod(unit, TILES)
            x_rows = x_pool.tile([P, K], BF16)
            nc.sync.dma_start(out=x_rows[:], in_=x[n].rearrange("(t j) k -> t j k", j=TILES)[:, j, :])
            x_rows_of[unit] = x_rows

        zero = const.tile([P, 1], F32)
        nc.vector.memset(zero[:], 0.0)
        one = const.tile([P, 1], F32)
        nc.scalar.activation(out=one[:], in_=zero[:], func=ACT.Exp)
        ident = const.tile([P, P], F32)
        make_identity(nc, ident[:])

        b_row = const.tile([P, QK_COLS], BF16)
        nc.vector.memset(b_row[:], 0.0)
        nc.sync.dma_start(out=b_row[0:1, :], in_=b_qk.rearrange("(o n) -> o n", o=1))
        ones = const.tile([P, P], BF16)
        nc.vector.memset(ones[:], 1.0)
        k_bias = const.tile([P, Q_COLS], F32)
        q_bias = const.tile([P, Q_BLOCKS], F32)

        def make_biases():
            k_bias_sum = psum_q.tile([P, Q_COLS], F32, name="q")
            nc.tensor.matmul(
                out=k_bias_sum[:], lhsT=ones[:], rhs=b_row[:, Q_COLS:QK_COLS], start=True, stop=True
            )
            nc.scalar.copy(
                out=k_bias[:].rearrange("p (d g) -> p d g", d=HD),
                in_=k_bias_sum[:].rearrange("p (g d) -> p d g", d=HD),
            )
            q_bias_sum = psum_q.tile([P, Q_BLOCKS, P], F32, name="q")
            for b in range(Q_BLOCKS):
                nc.tensor.matmul(
                    out=q_bias_sum[:, b, :],
                    lhsT=b_row[:, b * P : (b + 1) * P],
                    rhs=ones[:],
                    start=True,
                    stop=True,
                )
            nc.scalar.activation(
                out=q_bias[:], in_=q_bias_sum[:, :, 0], func=ACT.Copy, scale=-(HD**-0.5)
            )

        w_codes = const.tile([P, PASSES, QK_COLS], U32, align_bytes=64)
        w_scales = const.tile([P, PASSES, QK_COLS], U8, align_bytes=64)
        w_rows_of = {}
        for c in range(PASSES):
            w_rows = const.tile([P, PACK, QK_COLS], BF16, name="w_rows%d" % c)
            first = c * PACK * P
            nc.sync.dma_start(
                out=w_rows[:],
                in_=w_qk[first : first + PACK * P, :].rearrange("(p v) n -> p v n", v=PACK),
            )
            w_rows_of[c] = w_rows
            load_x(c)

        for unit in range(PASSES, LOAD_AHEAD):
            load_x(unit)

        def prepare_weights():
            for c in range(PASSES):
                w_grouped = const.tile(
                    [P, QK_COLS, PACK], BF16, align_bytes=64, name="w_grouped%d" % c
                )
                nc.vector.tensor_copy(
                    out=w_grouped[:], in_=w_rows_of[c][:].rearrange("p v n -> p n v")
                )
                nc.vector.quantize_mx(
                    out=w_codes[:, c, :].bitcast(FP8X4),
                    scales=w_scales[:, c, :],
                    in_=w_grouped[:].rearrange("p n v -> p (n v)"),
                )

        def sort_x(unit):
            x_sorted = work.tile([P, PASSES, 2, P], F32)
            nc.scalar.copy(
                out=x_sorted[:],
                in_=x_rows_of[unit][:].bitcast(F32).rearrange("t (c p u) -> t c u p", c=PASSES, u=2),
            )
            x_sorted_of[unit] = x_sorted

        def turn_x(unit):
            x_turned = psum_turns.tile([P, WORD_TILES, P], F32, name="turn")
            for w in range(WORD_TILES):
                c, u = divmod(w, 2)
                if unit < UNSORTED:
                    words = x_rows_of[unit][:].bitcast(F32)[:, 2 * P * c + u : 2 * P * (c + 1) : 2]
                else:
                    words = x_sorted_of[unit][:, c, u, :]
                nc.tensor.transpose(x_turned[:, w, :], words, ident[:])
            if unit % PAIR == 0:
                x_grouped = work.tile([P, PASSES, PAIR, P * PACK], BF16, align_bytes=64)
                x_grouped_of[unit // PAIR] = x_grouped
            nc.scalar.copy(
                out=x_grouped_of[unit // PAIR][:, :, unit % PAIR, :]
                .bitcast(F32)
                .rearrange("p c (t u) -> p c t u", u=2),
                in_=x_turned[:].rearrange("p (c u) t -> p c t u", u=2),
            )

        def quantise_x(pair):
            x_codes = work.tile([P, PASSES, PAIR * P], U32, align_bytes=64)
            x_scales = work.tile([P, PASSES, PAIR * P], U8, align_bytes=64)
            nc.vector.quantize_mx(
                out=x_codes[:].rearrange("p c t -> p (c t)").bitcast(FP8X4),
                scales=x_scales[:].rearrange("p c t -> p (c t)"),
                in_=x_grouped_of[pair][:].rearrange("p c j w -> p (c j w)"),
            )
            x_mx_of[pair] = (x_codes, x_scales)

        def project(pair):
            x_codes, x_scales = x_mx_of[pair]
            q_rows_sum = psum_turns.tile([P, Q_BLOCKS, PAIR * P], F32, name="turn")
            for b in range(Q_BLOCKS):
                for c in range(PASSES):
                    nc.tensor.matmul_mx(
                        out=q_rows_sum[:, b, :],
                        lhsT=w_codes[:, c, b * P : (b + 1) * P].bitcast(FP8X4),
                        lhsT_scale=w_scales[:, c, b * P : (b + 1) * P],
                        rhs=x_codes[:, c, :].bitcast(FP8X4),
                        rhs_scale=x_scales[:, c, :],
                        start=(c == 0),
                        stop=(c == PASSES - 1),
                    )
            q_rows_sum_of[pair] = q_rows_sum
            k_sum = psum_turns.tile([P, PAIR, Q_COLS], F32, name="turn")
            for j in range(PAIR):
                for c in range(PASSES):
                    nc.tensor.matmul_mx(
                        out=k_sum[:, j, :],
                        lhsT=x_codes[:, c, j * P : (j + 1) * P].bitcast(FP8X4),
                        lhsT_scale=x_scales[:, c, j * P : (j + 1) * P],
                        rhs=w_codes[:, c, Q_COLS:QK_COLS].bitcast(FP8X4),
                        rhs_scale=w_scales[:, c, Q_COLS:QK_COLS],
                        start=(c == 0),
                        stop=(c == PASSES - 1),
                    )
            k_sum_of[pair] = k_sum

        def add_q_bias(pair):
            q_rows = work.tile([P, Q_BLOCKS, PAIR * P], F32)
            for b in range(Q_BLOCKS):
                nc.scalar.activation(
                    out=q_rows[:, b, :],
                    in_=q_rows_sum_of[pair][:, b, :],
                    func=ACT.Identity,
                    bias=q_bias[:, b : b + 1],
                    scale=-(HD**-0.5),
                )
            q_rows_of[pair] = q_rows

        def turn_q(unit):
            q = psum_q.tile([P, Q_COLS], F32)
            tokens = slice(unit % PAIR * P, (unit % PAIR + 1) * P)
            for b in range(Q_BLOCKS):
                nc.tensor.transpose(
                    q[:, b * P : (b + 1) * P], q_rows_of[unit // PAIR][:, b, tokens], ident[:]
                )
            q_of[unit] = q[:].rearrange("p (h d) -> p d h", d=HD)

        def keep_last_q(unit):
            q_kept = work.tile([P, D_ON_GPSIMD, HEADS], F32)
            nc.scalar.copy(out=q_kept[:], in_=q_of[unit][:, D_ON_VECTOR:, :])
            q_kept_of[unit] = q_kept

        def add_k_bias(pair):
            k = work.tile([P, PAIR, HD, HEADS], F32)
            for_each = k_bias[:].rearrange("p (d g) -> p d g", d=HD).unsqueeze(1)
            nc.vector.tensor_tensor(
                out=k[:],
                in0=k_sum_of[pair][:].rearrange("p j (g d) -> p j d g", d=HD),
                in1=for_each.to_broadcast([P, PAIR, HD, HEADS]),
                op=ALU.add,
            )
            k_of[pair] = k

        def heads_of(blocks):
            return slice(blocks[0] * HEADS_PER_BLOCK, (blocks[-1] + 1) * HEADS_PER_BLOCK)

        def multiply(engine, products, q, k):
            shape = products[:].shape
            engine.tensor_tensor(
                out=products[:],
                in0=q.unsqueeze(3).to_broadcast(shape),
                in1=k.unsqueeze(2).to_broadcast(shape),
                op=ALU.mult,
            )

        def multiply_heads(unit, blocks):
            heads = heads_of(blocks)
            products = work.tile(
                [P, D_ON_VECTOR, heads.stop - heads.start, HEADS], F32, name="products" + tag(blocks)
            )
            q = q_of[unit][:, :D_ON_VECTOR, heads]
            multiply(nc.vector, products, q, k_of[unit // PAIR][:, unit % PAIR, :D_ON_VECTOR, :])
            products_of[unit, blocks] = products

        def multiply_last_d(unit, blocks):
            heads = heads_of(blocks)
            last_products = work.tile(
                [P, D_ON_GPSIMD, heads.stop - heads.start, HEADS], F32, name="last" + tag(blocks)
            )
            q = q_kept_of[unit][:, :, heads]
            multiply(nc.gpsimd, last_products, q, k_of[unit // PAIR][:, unit % PAIR, D_ON_VECTOR:, :])
            last_products_of[unit, blocks] = last_products

        def sum_over_d(unit, blocks):
            pair_rows = {b: psum_turns.tile([P, P], F32, name="turn") for b in blocks}
            terms = [products_of[unit, blocks][:, d, :, :] for d in range(D_ON_VECTOR)]
            terms += [last_products_of[unit, blocks][:, i, :, :] for i in range(D_ON_GPSIMD)]
            for i, term in enumerate(terms):
                for j, b in enumerate(blocks):
                    h0 = j * HEADS_PER_BLOCK
                    nc.tensor.matmul(
                        out=pair_rows[b][:],
                        lhsT=term[:, h0 : h0 + HEADS_PER_BLOCK, :].rearrange("p h g -> p (h g)"),
                        rhs=ident[:],
                        is_transpose=True,
                        start=(i == 0),
                        stop=(i == len(terms) - 1),
                    )
            pair_rows_of[unit, blocks] = pair_rows

        def keep_pair_rows(unit, blocks):
            pair_rows_kept = work.tile([P, len(blocks), P], F32, name="kept" + tag(blocks))
            copy = nc.scalar.copy if blocks == ALL_BLOCKS else nc.vector.tensor_copy
            for j, b in enumerate(blocks):
                copy(out=pair_rows_kept[:, j, :], in_=pair_rows_of[unit, blocks][b][:])
            pair_rows_kept_of[unit, blocks] = pair_rows_kept

        def turn_back(unit, blocks):
            heads = heads_of(blocks)
            score = psum_turns.tile([P, heads.stop - heads.start, HEADS], F32, name="turn")
            for j in range(len(blocks)):
                h0 = j * HEADS_PER_BLOCK
                nc.tensor.transpose(
                    score[:, h0 : h0 + HEADS_PER_BLOCK, :].rearrange("p h g -> p (h g)"),
                    pair_rows_kept_of[unit, blocks][:, j, :],
                    ident[:],
                )
            score_of[unit, blocks] = score

        def find_low(unit, blocks):
            heads = heads_of(blocks)
            low = soft_pool.tile([P, heads.stop - heads.start], F32, name="low" + tag(blocks))
            nc.vector.tensor_reduce(
                out=low[:], in_=score_of[unit, blocks][:], axis=AXIS.X, op=ALU.min
            )
            low_of[unit, blocks] = low

        def exponential(unit, blocks):
            heads = heads_of(blocks)
            count = heads.stop - heads.start
            prob = soft_pool.tile([P, count, HEADS], F32, name="prob" + tag(blocks))
            if unit >= LAST_SCALED:
                total = soft_pool.tile([P, count], F32, name="total" + tag(blocks))
            else:
                if unit % PAIR == 0:
                    totals_of[unit // PAIR] = soft_pool.tile([P, PAIR, count], F32, name="totals")
                total = totals_of[unit // PAIR][:, unit % PAIR, :]
            for h in range(count):
                nc.scalar.activation(
                    out=prob[:, h, :],
                    in_=score_of[unit, blocks][:, h, :],
                    func=ACT.Exp,
                    bias=low_of[unit, blocks][:, h : h + 1],
                    scale=-1.0,
                    accum_out=total[:, h : h + 1],
                )
            prob_of[unit, blocks] = prob
            total_of[unit, blocks] = total

        def invert(unit, blocks):
            heads = heads_of(blocks)
            if unit < LAST_SCALED:
                if unit % PAIR == PAIR - 1:
                    inverses = soft_pool.tile([P, PAIR, HEADS], F32)
                    nc.vector.reciprocal(out=inverses[:], in_=totals_of[unit // PAIR][:])
                    for j in range(PAIR):
                        inverse_of[unit - unit % PAIR + j] = inverses[:, j, :]
                return
            inverse = soft_pool.tile([P, heads.stop - heads.start], F32, name="inverse" + tag(blocks))
            nc.vector.reciprocal(out=inverse[:], in_=total_of[unit, blocks][:])
            prob = prob_of[unit, blocks]
            nc.vector.tensor_tensor(
                out=prob[:],
                in0=prob[:],
                in1=inverse[:].unsqueeze(2).to_broadcast(prob[:].shape),
                op=ALU.mult,
            )
            store(unit, blocks)

        def scale_and_store(unit, blocks):
            if unit >= LAST_SCALED:
                return
            prob = prob_of[unit, blocks]
            for h in range(HEADS):
                nc.scalar.activation(
                    out=prob[:, h, :],
                    in_=prob[:, h, :],
                    func=ACT.Copy,
                    scale=inverse_of[unit][:, h : h + 1],
                )
            store(unit, blocks)

        def store(unit, blocks):
            n, j = divmod(unit, TILES)
            nc.sync.dma_start(
                out=out[n].rearrange("(t j) h g -> t j h g", j=TILES)[:, j, heads_of(blocks), :],
                in_=prob_of[unit, blocks][:],
            )

        def tag(blocks):
            return "" if blocks == ALL_BLOCKS else "_of_block"

        def run(stage, unit):
            if 0 <= unit < UNITS:
                stage(unit)

        def run_blocks(stage, unit):
            if 0 <= unit < UNITS:
                for blocks in BLOCK_BY_BLOCK if unit == UNITS - 1 else [ALL_BLOCKS]:
                    stage(unit, blocks)

        def run_pair(stage, unit):
            if 0 <= unit < UNITS and unit % PAIR == 0:
                stage(unit // PAIR)

        make_biases()
        for step in range(UNITS + NORMALISE_LAG):
            run(load_x, step + LOAD_AHEAD)
            run(turn_q, step - MULTIPLY_LAG)
            run_blocks(keep_pair_rows, step - BACK_LAG)
            run(keep_last_q, step - MULTIPLY_LAG)
            run_blocks(scale_and_store, step - NORMALISE_LAG)
            run_pair(add_k_bias, step - MULTIPLY_LAG)
            run_pair(quantise_x, step - QUANTISE_LAG)
            run_blocks(invert, step - INVERT_LAG)
            run_blocks(multiply_last_d, step - MULTIPLY_LAG)
            run_blocks(find_low, step - SHIFT_LAG)
            run_blocks(multiply_heads, step - MULTIPLY_LAG)
            run_pair(project, step - PROJECT_LAG)
            if step + SORT_AHEAD >= UNSORTED:
                run(sort_x, step + SORT_AHEAD)
            run_blocks(exponential, step - SHIFT_LAG)
            run_pair(add_q_bias, step - PROJECT_LAG)
            run(turn_x, step)
            if step == 0:
                prepare_weights()
            run_blocks(sum_over_d, step - SUM_LAG)
            run_blocks(turn_back, step - BACK_LAG)
